import numpy as np
import ml_dtypes


def mxq(x, axis, fmt="e4m3"):
    dtype, down = {"e4m3": (ml_dtypes.float8_e4m3fn, 7), "e5m2": (ml_dtypes.float8_e5m2, 14)}[fmt]
    v = np.moveaxis(np.asarray(x, np.float32).astype(ml_dtypes.bfloat16).astype(np.float64), axis, -1)
    blocks = v.reshape(v.shape[:-1] + (-1, 32))
    amax = np.abs(blocks).max(-1, keepdims=True)
    byte = np.maximum(np.where(amax > 0, np.frexp(amax)[1] - 1 + 127, 0) - down, 1)
    scale = np.exp2(byte - 127.0)
    codes = (blocks / scale).astype(np.float32).astype(dtype).astype(np.float64)
    return np.moveaxis((codes * scale).reshape(v.shape), -1, axis)


WIDE = False


def mx_kscale(k):
    if not WIDE:
        return np.ones(k)
    levels = np.array([10, -10, 5, -5, 0])
    a = np.random.permutation(np.resize(levels, k // 512 * 4)).reshape(k // 512, 4)
    idx = np.arange(k)
    return np.exp2(a[idx // 512, idx % 128 // 32])


BF16 = ml_dtypes.bfloat16


def bf(x):
    return np.asarray(x, np.float32).astype(BF16)


def f64(x):
    return np.asarray(x).astype(np.float64)


E2M1 = np.array([0.0, 0.5, 1.0, 1.5, 2.0, 3.0, 4.0, 6.0, -0.0, -0.5, -1.0, -1.5, -2.0, -3.0, -4.0, -6.0])


def pack_weight(w, fmt):
    k, n = w.shape
    w = f64(bf(w)).reshape(k // 32, 32, n)
    amax = np.abs(w).max(1)
    if fmt == "e4m3":
        byte = np.frexp(amax)[1] - 1 + 127 - 7
    else:
        mant, ex = np.frexp(amax / 6.0)
        byte = np.where(mant > 0.5, ex, ex - 1) + 127
    byte = np.clip(np.where(amax > 0, byte, 1), 1, 254)
    scaled = (w * np.exp2(127.0 - byte)[:, None, :]).reshape(k, n).astype(np.float32)
    by_word = np.ascontiguousarray(scaled.reshape(k // 512, 128, 4, n).transpose(0, 1, 3, 2))
    if fmt == "e4m3":
        words = by_word.astype(ml_dtypes.float8_e4m3fn).view(np.uint8)
    else:
        c = by_word.astype(ml_dtypes.float4_e2m1fn).view(np.uint8) & 0xF
        words = c[..., 0::2] | (c[..., 1::2] << 4)
    return np.ascontiguousarray(words), np.ascontiguousarray(byte.astype(np.uint8).reshape(k // 512, 16, n))


def unpack_weight(words, scales, fmt):
    g, p, n, _ = words.shape
    if fmt == "e4m3":
        vals = np.ascontiguousarray(words).view(ml_dtypes.float8_e4m3fn).astype(np.float64)
    else:
        nib = np.empty((g, p, n, 4), np.uint8)
        nib[..., 0::2] = words & 0xF
        nib[..., 1::2] = words >> 4
        vals = E2M1[nib]
    vals = vals * np.repeat(np.exp2(scales.astype(np.float64) - 127.0), 8, axis=1)[..., None]
    return vals.transpose(0, 1, 3, 2).reshape(g * 512, n)


B, CH, CQ, CV, H, W = 4, 512, 128, 256, 32, 64
EPS = 1e-5
POOL = 2
HW = H * W
HW4 = HW // (POOL * POOL)
A = 1.5 / CQ ** 0.25
FMT = "e4m3"


def bn(y, s, b, m, v):
    inv = f64(s) / np.sqrt(f64(v) + EPS)
    return y * inv[None, :, None] + (f64(b) - f64(m) * inv)[None, :, None]


def maxpool(y):
    c = y.shape[1]
    return y.reshape(B, c, H // POOL, POOL, W // POOL, POOL).max(axis=(3, 5)).reshape(B, c, HW4)


def vec(c, z):
    return bf(z * np.random.standard_normal(c))


def pos(c):
    return bf(0.5 + np.random.random(c))


def setup_inputs():
    s = mx_kscale(CH)
    out = {'memory': bf(np.random.standard_normal((B, CH, H, W)) * s[None, :, None, None])}
    out['wq_words'], out['wq_scales'] = pack_weight((np.random.standard_normal((CQ, CH)) * A / np.sqrt(CH) / s).T, FMT)
    out.update({'bq': vec(CQ, 0.1),
                'bnq_s': pos(CQ), 'bnq_b': vec(CQ, 0.1), 'bnq_m': vec(CQ, 0.1), 'bnq_v': pos(CQ)})
    out['wk_words'], out['wk_scales'] = pack_weight((np.random.standard_normal((CQ, CH)) * A / np.sqrt(CH) / s).T, FMT)
    out.update({'bk': vec(CQ, 0.1),
                'bnk_s': pos(CQ), 'bnk_b': vec(CQ, 0.1), 'bnk_m': vec(CQ, 0.1), 'bnk_v': pos(CQ)})
    out['wv_words'], out['wv_scales'] = pack_weight((np.random.standard_normal((CV, CH)) / np.sqrt(CH) / s).T, FMT)
    out.update({'bv': vec(CV, 0.3),
                'bnv_s': pos(CV), 'bnv_b': vec(CV, 0.3), 'bnv_m': vec(CV, 0.3), 'bnv_v': pos(CV)})
    return out


def reference(memory, wq_words, wq_scales, bq, bnq_s, bnq_b, bnq_m, bnq_v, wk_words, wk_scales, bk, bnk_s, bnk_b, bnk_m, bnk_v, wv_words, wv_scales, bv, bnv_s, bnv_b, bnv_m, bnv_v):
    mq = mxq(f64(memory).reshape(B, CH, HW), 1, 'e4m3')
    yq = (unpack_weight(wq_words, wq_scales, FMT).T @ mq) + f64(bq)[None, :, None]
    yk = (unpack_weight(wk_words, wk_scales, FMT).T @ mq) + f64(bk)[None, :, None]
    yv = (unpack_weight(wv_words, wv_scales, FMT).T @ mq) + f64(bv)[None, :, None]
    q = bn(yq, bnq_s, bnq_b, bnq_m, bnq_v).transpose(0, 2, 1)
    k = maxpool(bn(yk, bnk_s, bnk_b, bnk_m, bnk_v))
    v = maxpool(bn(yv, bnv_s, bnv_b, bnv_m, bnv_v)).transpose(0, 2, 1)
    return q, k, v

@@ -1,0 +1,196 @@
+from contextlib import ExitStack
+
+import concourse.mybir as mybir
+from concourse.masks import make_identity
+
+F32 = mybir.dt.float32
+BF16 = mybir.dt.bfloat16
+I32 = mybir.dt.int32
+U32 = mybir.dt.uint32
+U8 = mybir.dt.uint8
+FP8X4 = mybir.dt.float8_e4m3fn_x4
+ALU = mybir.AluOpType
+FUNC = mybir.ActivationFunctionType
+
+P = 128
+PACK = 4
+B, CH, H, W = 4, 512, 32, 64
+HW = H * W
+POOLED = HW // 4
+MEMBERS = 4
+C_OUT = 512
+GROUPS = C_OUT // P
+Q, K, V_LOW, V_HIGH = 0, 1, 2, 3
+R = POOLED // P
+EPS = 1e-5
+HALVES = 2
+LEAD = 3
+SMALL_LOADS_PER_IMAGE = 6
+
+FLOPS = 2 * B * HW * CH * C_OUT
+
+
+def tile_selfattention_pa_t_kernel(
+    tc,
+    memory,
+    wq_words, wq_scales, bq, bnq_s, bnq_b, bnq_m, bnq_v,
+    wk_words, wk_scales, bk, bnk_s, bnk_b, bnk_m, bnk_v,
+    wv_words, wv_scales, bv, bnv_s, bnv_b, bnv_m, bnv_v,
+    out_0, out_1, out_2,
+):
+    nc = tc.nc
+    with ExitStack() as ctx:
+        keep = ctx.enter_context(tc.tile_pool(name="keep", bufs=1))
+        stage = ctx.enter_context(tc.tile_pool(name="stage", bufs=2))
+        results = ctx.enter_context(tc.tile_pool(name="results", bufs=3))
+        psum_acc = ctx.enter_context(tc.psum_pool(name="psum_acc", bufs=5))
+        psum_tp = ctx.enter_context(tc.psum_pool(name="psum_tp", bufs=3))
+
+        raw = [keep.tile([P, PACK, HW], BF16, name="raw%d" % b) for b in range(B)]
+        codes = [keep.tile([P, MEMBERS, POOLED], U32, align_bytes=64, name="codes%d" % b) for b in range(B)]
+        scales = [keep.tile([P, MEMBERS, POOLED], U8, align_bytes=64, name="scales%d" % b) for b in range(B)]
+        w_codes = keep.tile([P, C_OUT], U32, align_bytes=64)
+        w_scales = keep.tile([P, C_OUT], U8, align_bytes=64)
+        vectors = keep.tile([P, P], BF16)
+        ident = keep.tile([P, P], F32)
+
+        nc.vector.memset(w_scales[:].bitcast(I32), 0)
+        nc.vector.memset(vectors[:], 0.0)
+        make_identity(nc, ident[:])
+
+        small_loads = []
+        by_kind = ((bq, bk, bv), (bnq_s, bnk_s, bnv_s), (bnq_b, bnk_b, bnv_b), (bnq_m, bnk_m, bnv_m), (bnq_v, bnk_v, bnv_v))
+        for kind, (of_q, of_k, of_v) in enumerate(by_kind):
+            row = GROUPS * kind
+            small_loads.append((vectors[row + Q : row + Q + 1, :], of_q.rearrange("(o c) -> o c", o=1)))
+            small_loads.append((vectors[row + K : row + K + 1, :], of_k.rearrange("(o c) -> o c", o=1)))
+            small_loads.append((vectors[row + V_LOW : row + V_HIGH + 1, :], of_v.rearrange("(o c) -> o c", o=2)))
+        for words, scale_rows, first, width in ((wq_words, wq_scales, 0, P), (wk_words, wk_scales, P, P), (wv_words, wv_scales, 2 * P, 2 * P)):
+            cols = slice(first, first + width)
+            small_loads.append((w_codes[:, cols].bitcast(I32), words[0].rearrange("p n t -> p (n t)").bitcast(I32)))
+            for a in range(4):
+                small_loads.append((w_scales[32 * a : 32 * a + 4, cols].bitcast(I32), scale_rows[0, 4 * a : 4 * a + 4, :].bitcast(I32)))
+
+        for b in range(B):
+            image = memory[b].rearrange("(p t) h w -> p t (h w)", t=PACK)
+            for s in range(HALVES):
+                part = slice(s * HW // HALVES, (s + 1) * HW // HALVES)
+                nc.sync.dma_start(out=raw[b][:, :, part], in_=image[:, :, part])
+            last = len(small_loads) if b == B - 1 else (b + 1) * SMALL_LOADS_PER_IMAGE
+            for dst, src in small_loads[b * SMALL_LOADS_PER_IMAGE : last]:
+                nc.sync.dma_start(out=dst, in_=src)
+
+        def prepare(b):
+            grouped = [stage.tile([P, POOLED, PACK], BF16, align_bytes=64, name="grouped%d" % j) for j in range(MEMBERS)]
+            by_member = raw[b][:].rearrange("p t (hh dh ww dw) -> p dh dw hh ww t", dh=2, ww=W // 2, dw=2)
+            for s in range(HALVES):
+                rows = slice(s * H // 4, (s + 1) * H // 4)
+                for j in range(MEMBERS):
+                    dh, dw = divmod(j, 2)
+                    copy = nc.vector.tensor_copy if dw == 0 else nc.scalar.copy
+                    copy(
+                        out=grouped[j][:].rearrange("p (hh ww) t -> p hh ww t", ww=W // 2)[:, rows, :, :],
+                        in_=by_member[:, dh, dw, rows, :, :],
+                    )
+            for j in range(MEMBERS):
+                nc.vector.quantize_mx(
+                    out=codes[b][:, j, :].bitcast(FP8X4),
+                    scales=scales[b][:, j, :],
+                    in_=grouped[j][:].rearrange("p c t -> p (c t)"),
+                )
+
+        def batch_norm_constants():
+            vectors_f32 = keep.tile([P, P], F32)
+            nc.vector.tensor_copy(out=vectors_f32[:], in_=vectors[:])
+            turned = psum_tp.tile([P, P], F32, tag="tp")
+            nc.tensor.transpose(turned[:], vectors_f32[:], ident[:])
+            bn = keep.tile([P, 5, GROUPS], F32)
+            nc.vector.tensor_copy(out=bn[:].rearrange("p k g -> p (k g)"), in_=turned[:, 0 : 5 * GROUPS])
+            bias, gain, beta, mean, var = (bn[:, kind, :] for kind in range(5))
+            inv = keep.tile([P, GROUPS], F32)
+            shift = keep.tile([P, GROUPS], F32)
+            nc.vector.tensor_scalar_add(out=inv[:], in0=var, scalar1=EPS)
+            nc.scalar.sqrt(out=inv[:], in_=inv[:])
+            nc.vector.reciprocal(out=inv[:], in_=inv[:])
+            nc.vector.tensor_mul(out=inv[:], in0=inv[:], in1=gain)
+            nc.vector.tensor_sub(out=shift[:], in0=bias, in1=mean)
+            nc.vector.tensor_mul(out=shift[:], in0=shift[:], in1=inv[:])
+            nc.vector.tensor_add(out=shift[:], in0=shift[:], in1=beta)
+            spread = psum_tp.tile([P, 2 * P], F32, tag="tp")
+            for half, g in enumerate((V_LOW, V_HIGH)):
+                nc.tensor.matmul(
+                    out=spread[:, half * P : (half + 1) * P],
+                    lhsT=shift[:, g : g + 1].to_broadcast([P, P]),
+                    rhs=ident[:],
+                    start=True,
+                    stop=True,
+                )
+            shift_v = keep.tile([P, 2 * P], F32)
+            nc.vector.tensor_copy(out=shift_v[:], in_=spread[:])
+            return inv, shift, shift_v
+
+        def produce(b, inv, shift, shift_v):
+            q_rows = out_0[b].rearrange("(hh dh wq x) c -> dh hh wq (x c)", dh=2, wq=W // 8, x=8)
+            pooled = {g: results.tile([P, POOLED], F32, name="pooled%d" % g) for g in (K, V_LOW, V_HIGH)}
+            zq = {}
+            for j in range(MEMBERS):
+                dh, dw = divmod(j, 2)
+                for g in range(GROUPS):
+                    acc = psum_acc.tile([P, POOLED], F32, tag="acc")
+                    nc.tensor.matmul_mx(
+                        out=acc[:],
+                        lhsT=w_codes[:, g * P : (g + 1) * P].bitcast(FP8X4),
+                        lhsT_scale=w_scales[:, g * P : (g + 1) * P],
+                        rhs=codes[b][:, j, :].bitcast(FP8X4),
+                        rhs_scale=scales[b][:, j, :],
+                        start=True,
+                        stop=True,
+                    )
+                    y = acc[:] if g == K else acc[:].rearrange("c (u r) -> c r u", r=R)
+                    if g == Q:
+                        zq[dw] = results.tile([P, R, P], F32, name="zq", bufs=4)
+                        nc.scalar.activation(out=zq[dw][:], in_=y, func=FUNC.Identity, scale=inv[:, g : g + 1], bias=shift[:, g : g + 1])
+                    else:
+                        best = pooled[g][:] if g == K else pooled[g][:].rearrange("c (r u) -> c r u", r=R)
+                        if j == 0:
+                            nc.scalar.activation(out=best, in_=y, func=FUNC.Copy, scale=inv[:, g : g + 1])
+                        else:
+                            nc.vector.scalar_tensor_tensor(out=best, in0=y, scalar=inv[:, g : g + 1], in1=best, op0=ALU.mult, op1=ALU.max)
+                if dw == 1:
+                    q_out = results.tile([P, R, 2, P], F32)
+                    for pair in range(R // 2):
+                        turned = psum_tp.tile([P, 2, 2, P], F32, tag="tp")
+                        for i in range(2):
+                            for d in range(2):
+                                nc.tensor.transpose(turned[:, i, d, :], zq[d][:, 2 * pair + i, :], ident[:])
+                        nc.scalar.copy(out=q_out[:, 2 * pair : 2 * pair + 2, :, :], in_=turned[:])
+                    nc.sync.dma_start(out=q_rows[dh], in_=q_out[:].rearrange("u r d c -> u (r d c)"))
+
+            nc.vector.tensor_scalar_add(out=pooled[K][:], in0=pooled[K][:], scalar1=shift[:, K : K + 1])
+            nc.sync.dma_start(out=out_1[b], in_=pooled[K][:])
+
+            v_out = results.tile([P, R, 2 * P], F32)
+            for pair in range(R // 2):
+                turned = psum_tp.tile([P, 2, 2 * P], F32, tag="tp")
+                for i in range(2):
+                    for half, g in enumerate((V_LOW, V_HIGH)):
+                        nc.tensor.transpose(
+                            turned[:, i, half * P : (half + 1) * P],
+                            pooled[g][:, (2 * pair + i) * P : (2 * pair + i + 1) * P],
+                            ident[:],
+                        )
+                nc.vector.tensor_tensor(
+                    out=v_out[:, 2 * pair : 2 * pair + 2, :],
+                    in0=turned[:],
+                    in1=shift_v[:].unsqueeze(1).to_broadcast([P, 2, 2 * P]),
+                    op=ALU.add,
+                )
+            nc.sync.dma_start(out=out_2[b].rearrange("(u r) c -> u (r c)", r=R), in_=v_out[:].rearrange("u r c -> u (r c)"))
+
+        for b in range(LEAD):
+            prepare(b)
+        inv, shift, shift_v = batch_norm_constants()
+        for b in range(B):
+            produce(b, inv, shift, shift_v)
+            if b + LEAD < B:
+                prepare(b + LEAD)

@@ -18,14 +18,17 @@ B, CH, H, W = 4, 512, 32, 64
 HW = H * W
 POOLED = HW // 4
 MEMBERS = 4
+EVEN_COLUMNS = (0, 2)
+ODD_COLUMNS = (1, 3)
 C_OUT = 512
 GROUPS = C_OUT // P
 Q, K, V_LOW, V_HIGH = 0, 1, 2, 3
 R = POOLED // P
 EPS = 1e-5
-HALVES = 2
+PIECES = 2
+FIRST_IMAGE_PIECES = 4
+SMALL_LOADS_PER_PAIR = 6
 LEAD = 3
-SMALL_LOADS_PER_IMAGE = 6
 
 FLOPS = 2 * B * HW * CH * C_OUT
 
@@ -45,6 +48,7 @@ def tile_selfattention_pa_t_kernel(
         results = ctx.enter_context(tc.tile_pool(name="results", bufs=3))
         psum_acc = ctx.enter_context(tc.psum_pool(name="psum_acc", bufs=5))
         psum_tp = ctx.enter_context(tc.psum_pool(name="psum_tp", bufs=3))
+        ctx.enter_context(tc.manual_schedule())
 
         raw = [keep.tile([P, PACK, HW], BF16, name="raw%d" % b) for b in range(B)]
         codes = [keep.tile([P, MEMBERS, POOLED], U32, align_bytes=64, name="codes%d" % b) for b in range(B)]
@@ -53,50 +57,66 @@ def tile_selfattention_pa_t_kernel(
         w_scales = keep.tile([P, C_OUT], U8, align_bytes=64)
         vectors = keep.tile([P, P], BF16)
         ident = keep.tile([P, P], F32)
+        one = keep.tile([P, 1], F32)
 
         nc.vector.memset(w_scales[:].bitcast(I32), 0)
         nc.vector.memset(vectors[:], 0.0)
-        make_identity(nc, ident[:])
+        nc.vector.memset(one[:], 1.0)
+        nc.scalar.sqrt(out=one[:], in_=one[:])
 
-        small_loads = []
+        vector_loads = []
         by_kind = ((bq, bk, bv), (bnq_s, bnk_s, bnv_s), (bnq_b, bnk_b, bnv_b), (bnq_m, bnk_m, bnv_m), (bnq_v, bnk_v, bnv_v))
         for kind, (of_q, of_k, of_v) in enumerate(by_kind):
             row = GROUPS * kind
-            small_loads.append((vectors[row + Q : row + Q + 1, :], of_q.rearrange("(o c) -> o c", o=1)))
-            small_loads.append((vectors[row + K : row + K + 1, :], of_k.rearrange("(o c) -> o c", o=1)))
-            small_loads.append((vectors[row + V_LOW : row + V_HIGH + 1, :], of_v.rearrange("(o c) -> o c", o=2)))
+            vector_loads.append((vectors[row + Q : row + Q + 1, :], of_q.rearrange("(o c) -> o c", o=1)))
+            vector_loads.append((vectors[row + K : row + K + 1, :], of_k.rearrange("(o c) -> o c", o=1)))
+            vector_loads.append((vectors[row + V_LOW : row + V_HIGH + 1, :], of_v.rearrange("(o c) -> o c", o=2)))
+        for dst, src in vector_loads[:SMALL_LOADS_PER_PAIR]:
+            nc.gpsimd.dma_start(out=dst, in_=src)
+        make_identity(nc, ident[:])
+        small_loads = vector_loads[SMALL_LOADS_PER_PAIR:]
         for words, scale_rows, first, width in ((wq_words, wq_scales, 0, P), (wk_words, wk_scales, P, P), (wv_words, wv_scales, 2 * P, 2 * P)):
             cols = slice(first, first + width)
             small_loads.append((w_codes[:, cols].bitcast(I32), words[0].rearrange("p n t -> p (n t)").bitcast(I32)))
             for a in range(4):
                 small_loads.append((w_scales[32 * a : 32 * a + 4, cols].bitcast(I32), scale_rows[0, 4 * a : 4 * a + 4, :].bitcast(I32)))
 
-        for b in range(B):
-            image = memory[b].rearrange("(p t) h w -> p t (h w)", t=PACK)
-            for s in range(HALVES):
-                part = slice(s * HW // HALVES, (s + 1) * HW // HALVES)
-                nc.sync.dma_start(out=raw[b][:, :, part], in_=image[:, :, part])
-            last = len(small_loads) if b == B - 1 else (b + 1) * SMALL_LOADS_PER_IMAGE
-            for dst, src in small_loads[b * SMALL_LOADS_PER_IMAGE : last]:
-                nc.sync.dma_start(out=dst, in_=src)
+        def pieces_of(b):
+            return FIRST_IMAGE_PIECES if b == 0 else PIECES
 
-        def prepare(b):
-            grouped = [stage.tile([P, POOLED, PACK], BF16, align_bytes=64, name="grouped%d" % j) for j in range(MEMBERS)]
+        big_loads = [(b, s) for b in range(B) for s in range(pieces_of(b))]
+        assert len(small_loads) <= len(big_loads) // 2 * SMALL_LOADS_PER_PAIR
+        for n, (b, s) in enumerate(big_loads):
+            image = memory[b].rearrange("(p t) h w -> p t (h w)", t=PACK)
+            part = slice(s * HW // pieces_of(b), (s + 1) * HW // pieces_of(b))
+            nc.sync.dma_start(out=raw[b][:, :, part], in_=image[:, :, part])
+            if n % 2 == 1:
+                first = n // 2 * SMALL_LOADS_PER_PAIR
+                for dst, src in small_loads[first : first + SMALL_LOADS_PER_PAIR]:
+                    nc.sync.dma_start(out=dst, in_=src)
+
+        grouped = {}
+
+        def regroup(b):
+            for j in range(MEMBERS):
+                grouped[b, j] = stage.tile([P, POOLED, PACK], BF16, align_bytes=64, name="grouped%d" % j)
             by_member = raw[b][:].rearrange("p t (hh dh ww dw) -> p dh dw hh ww t", dh=2, ww=W // 2, dw=2)
-            for s in range(HALVES):
-                rows = slice(s * H // 4, (s + 1) * H // 4)
+            for s in range(pieces_of(b)):
+                rows = slice(s * (H // 2) // pieces_of(b), (s + 1) * (H // 2) // pieces_of(b))
                 for j in range(MEMBERS):
                     dh, dw = divmod(j, 2)
-                    copy = nc.vector.tensor_copy if dw == 0 else nc.scalar.copy
+                    copy = nc.vector.tensor_copy if j in EVEN_COLUMNS else nc.scalar.copy
                     copy(
-                        out=grouped[j][:].rearrange("p (hh ww) t -> p hh ww t", ww=W // 2)[:, rows, :, :],
+                        out=grouped[b, j][:].rearrange("p (hh ww) t -> p hh ww t", ww=W // 2)[:, rows, :, :],
                         in_=by_member[:, dh, dw, rows, :, :],
                     )
-            for j in range(MEMBERS):
+
+        def quantise(b, members):
+            for j in members:
                 nc.vector.quantize_mx(
                     out=codes[b][:, j, :].bitcast(FP8X4),
                     scales=scales[b][:, j, :],
-                    in_=grouped[j][:].rearrange("p c t -> p (c t)"),
+                    in_=grouped[b, j][:].rearrange("p c t -> p (c t)"),
                 )
 
         def batch_norm_constants():
@@ -129,46 +149,50 @@ def tile_selfattention_pa_t_kernel(
             nc.vector.tensor_copy(out=shift_v[:], in_=spread[:])
             return inv, shift, shift_v
 
-        def produce(b, inv, shift, shift_v):
-            q_rows = out_0[b].rearrange("(hh dh wq x) c -> dh hh wq (x c)", dh=2, wq=W // 8, x=8)
-            pooled = {g: results.tile([P, POOLED], F32, name="pooled%d" % g) for g in (K, V_LOW, V_HIGH)}
-            zq = {}
-            for j in range(MEMBERS):
-                dh, dw = divmod(j, 2)
-                for g in range(GROUPS):
-                    acc = psum_acc.tile([P, POOLED], F32, tag="acc")
-                    nc.tensor.matmul_mx(
-                        out=acc[:],
-                        lhsT=w_codes[:, g * P : (g + 1) * P].bitcast(FP8X4),
-                        lhsT_scale=w_scales[:, g * P : (g + 1) * P],
-                        rhs=codes[b][:, j, :].bitcast(FP8X4),
-                        rhs_scale=scales[b][:, j, :],
-                        start=True,
-                        stop=True,
-                    )
-                    y = acc[:] if g == K else acc[:].rearrange("c (u r) -> c r u", r=R)
-                    if g == Q:
-                        zq[dw] = results.tile([P, R, P], F32, name="zq", bufs=4)
-                        nc.scalar.activation(out=zq[dw][:], in_=y, func=FUNC.Identity, scale=inv[:, g : g + 1], bias=shift[:, g : g + 1])
+        zq = {}
+        pooled = {}
+
+        def multiply(b, j):
+            for g in range(GROUPS):
+                acc = psum_acc.tile([P, POOLED], F32, tag="acc")
+                nc.tensor.matmul_mx(
+                    out=acc[:],
+                    lhsT=w_codes[:, g * P : (g + 1) * P].bitcast(FP8X4),
+                    lhsT_scale=w_scales[:, g * P : (g + 1) * P],
+                    rhs=codes[b][:, j, :].bitcast(FP8X4),
+                    rhs_scale=scales[b][:, j, :],
+                    start=True,
+                    stop=True,
+                )
+                y = acc[:] if g == K else acc[:].rearrange("c (u r) -> c r u", r=R)
+                if g == Q:
+                    zq[b, j] = results.tile([P, R, P], F32, name="zq", bufs=4)
+                    nc.scalar.activation(out=zq[b, j][:], in_=y, func=FUNC.Identity, scale=inv[:, g : g + 1], bias=shift[:, g : g + 1])
+                else:
+                    if j == 0:
+                        pooled[b, g] = results.tile([P, POOLED], F32, name="pooled%d" % g)
+                    best = pooled[b, g][:] if g == K else pooled[b, g][:].rearrange("c (r u) -> c r u", r=R)
+                    if j == 0:
+                        nc.scalar.activation(out=best, in_=y, func=FUNC.Copy, scale=inv[:, g : g + 1])
                     else:
-                        best = pooled[g][:] if g == K else pooled[g][:].rearrange("c (r u) -> c r u", r=R)
-                        if j == 0:
-                            nc.scalar.activation(out=best, in_=y, func=FUNC.Copy, scale=inv[:, g : g + 1])
-                        else:
-                            nc.vector.scalar_tensor_tensor(out=best, in0=y, scalar=inv[:, g : g + 1], in1=best, op0=ALU.mult, op1=ALU.max)
-                if dw == 1:
-                    q_out = results.tile([P, R, 2, P], F32)
-                    for pair in range(R // 2):
-                        turned = psum_tp.tile([P, 2, 2, P], F32, tag="tp")
-                        for i in range(2):
-                            for d in range(2):
-                                nc.tensor.transpose(turned[:, i, d, :], zq[d][:, 2 * pair + i, :], ident[:])
-                        nc.scalar.copy(out=q_out[:, 2 * pair : 2 * pair + 2, :, :], in_=turned[:])
-                    nc.sync.dma_start(out=q_rows[dh], in_=q_out[:].rearrange("u r d c -> u (r d c)"))
+                        nc.vector.scalar_tensor_tensor(out=best, in0=y, scalar=inv[:, g : g + 1], in1=best, op0=ALU.mult, op1=ALU.max)
 
-            nc.vector.tensor_scalar_add(out=pooled[K][:], in0=pooled[K][:], scalar1=shift[:, K : K + 1])
-            nc.sync.dma_start(out=out_1[b], in_=pooled[K][:])
+        def store_q(b, dh):
+            q_out = results.tile([P, R, 2, P], F32)
+            for pair in range(R // 2):
+                turned = psum_tp.tile([P, 2, 2, P], F32, tag="tp")
+                for i in range(2):
+                    for dw in range(2):
+                        nc.tensor.transpose(turned[:, i, dw, :], zq[b, 2 * dh + dw][:, 2 * pair + i, :], ident[:])
+                nc.scalar.copy(out=q_out[:, 2 * pair : 2 * pair + 2, :, :], in_=turned[:])
+            q_rows = out_0[b].rearrange("(hh dh wq x) c -> dh hh wq (x c)", dh=2, wq=W // 8, x=8)
+            nc.sync.dma_start(out=q_rows[dh], in_=q_out[:].rearrange("u r d c -> u (r d c)"))
 
+        def store_k(b):
+            nc.vector.tensor_scalar_add(out=pooled[b, K][:], in0=pooled[b, K][:], scalar1=shift[:, K : K + 1])
+            nc.sync.dma_start(out=out_1[b], in_=pooled[b, K][:])
+
+        def store_v(b):
             v_out = results.tile([P, R, 2 * P], F32)
             for pair in range(R // 2):
                 turned = psum_tp.tile([P, 2, 2 * P], F32, tag="tp")
@@ -176,7 +200,7 @@ def tile_selfattention_pa_t_kernel(
                     for half, g in enumerate((V_LOW, V_HIGH)):
                         nc.tensor.transpose(
                             turned[:, i, half * P : (half + 1) * P],
-                            pooled[g][:, (2 * pair + i) * P : (2 * pair + i + 1) * P],
+                            pooled[b, g][:, (2 * pair + i) * P : (2 * pair + i + 1) * P],
                             ident[:],
                         )
                 nc.vector.tensor_tensor(
@@ -187,10 +211,28 @@ def tile_selfattention_pa_t_kernel(
                 )
             nc.sync.dma_start(out=out_2[b].rearrange("(u r) c -> u (r c)", r=R), in_=v_out[:].rearrange("u r c -> u (r c)"))
 
-        for b in range(LEAD):
-            prepare(b)
-        inv, shift, shift_v = batch_norm_constants()
-        for b in range(B):
-            produce(b, inv, shift, shift_v)
-            if b + LEAD < B:
-                prepare(b + LEAD)
+        def produce(b):
+            multiply(b, 0)
+            if b > 0:
+                store_q(b - 1, 1)
+            multiply(b, 1)
+            if b > 0:
+                store_v(b - 1)
+            multiply(b, 2)
+            store_q(b, 0)
+            multiply(b, 3)
+            store_k(b)
+
+        for step in range(B + LEAD):
+            if step == LEAD:
+                inv, shift, shift_v = batch_norm_constants()
+            if step >= LEAD:
+                produce(step - LEAD)
+            if step < B:
+                regroup(step)
+            if 1 <= step <= B:
+                quantise(step - 1, ODD_COLUMNS)
+            if step < B:
+                quantise(step, EVEN_COLUMNS)
+        store_q(B - 1, 1)
+        store_v(B - 1)

@@ -151,6 +151,7 @@ def tile_selfattention_pa_t_kernel(
 
         zq = {}
         pooled = {}
+        ordered = {}
 
         def multiply(b, j):
             for g in range(GROUPS):
@@ -164,18 +165,32 @@ def tile_selfattention_pa_t_kernel(
                     start=True,
                     stop=True,
                 )
-                y = acc[:] if g == K else acc[:].rearrange("c (u r) -> c r u", r=R)
                 if g == Q:
                     zq[b, j] = results.tile([P, R, P], F32, name="zq", bufs=4)
-                    nc.scalar.activation(out=zq[b, j][:], in_=y, func=FUNC.Identity, scale=inv[:, g : g + 1], bias=shift[:, g : g + 1])
+                    nc.scalar.activation(
+                        out=zq[b, j][:].rearrange("c r u -> c u r"),
+                        in_=acc[:].rearrange("c (u r) -> c u r", r=R),
+                        func=FUNC.Identity,
+                        scale=inv[:, g : g + 1],
+                        bias=shift[:, g : g + 1],
+                    )
+                elif j == 0:
+                    pooled[b, g] = results.tile([P, POOLED], F32, name="pooled%d" % g)
+                    nc.scalar.activation(out=pooled[b, g][:], in_=acc[:], func=FUNC.Copy, scale=inv[:, g : g + 1])
+                elif j < MEMBERS - 1 or g == K:
+                    nc.vector.scalar_tensor_tensor(
+                        out=pooled[b, g][:], in0=acc[:], scalar=inv[:, g : g + 1], in1=pooled[b, g][:], op0=ALU.mult, op1=ALU.max
+                    )
                 else:
-                    if j == 0:
-                        pooled[b, g] = results.tile([P, POOLED], F32, name="pooled%d" % g)
-                    best = pooled[b, g][:] if g == K else pooled[b, g][:].rearrange("c (r u) -> c r u", r=R)
-                    if j == 0:
-                        nc.scalar.activation(out=best, in_=y, func=FUNC.Copy, scale=inv[:, g : g + 1])
-                    else:
-                        nc.vector.scalar_tensor_tensor(out=best, in0=y, scalar=inv[:, g : g + 1], in1=best, op0=ALU.mult, op1=ALU.max)
+                    ordered[b, g] = results.tile([P, R, P], F32, name="ordered%d" % g)
+                    nc.vector.scalar_tensor_tensor(
+                        out=ordered[b, g][:].rearrange("c r u -> c u r"),
+                        in0=acc[:].rearrange("c (u r) -> c u r", r=R),
+                        scalar=inv[:, g : g + 1],
+                        in1=pooled[b, g][:].rearrange("c (u r) -> c u r", r=R),
+                        op0=ALU.mult,
+                        op1=ALU.max,
+                    )
 
         def store_q(b, dh):
             q_out = results.tile([P, R, 2, P], F32)
@@ -200,7 +215,7 @@ def tile_selfattention_pa_t_kernel(
                     for half, g in enumerate((V_LOW, V_HIGH)):
                         nc.tensor.transpose(
                             turned[:, i, half * P : (half + 1) * P],
-                            pooled[b, g][:, (2 * pair + i) * P : (2 * pair + i + 1) * P],
+                            ordered[b, g][:, 2 * pair + i, :],
                             ident[:],
                         )
                 nc.vector.tensor_tensor(

@@ -18,8 +18,7 @@ B, CH, H, W = 4, 512, 32, 64
 HW = H * W
 POOLED = HW // 4
 MEMBERS = 4
-EVEN_COLUMNS = (0, 2)
-ODD_COLUMNS = (1, 3)
+EVEN_ROWS, ODD_ROWS = 0, 1
 C_OUT = 512
 GROUPS = C_OUT // P
 Q, K, V_LOW, V_HIGH = 0, 1, 2, 3
@@ -28,7 +27,7 @@ EPS = 1e-5
 PIECES = 2
 FIRST_IMAGE_PIECES = 4
 SMALL_LOADS_PER_PAIR = 6
-LEAD = 3
+LEAD = 2
 
 FLOPS = 2 * B * HW * CH * C_OUT
 
@@ -85,39 +84,40 @@ def tile_selfattention_pa_t_kernel(
             return FIRST_IMAGE_PIECES if b == 0 else PIECES
 
         big_loads = [(b, s) for b in range(B) for s in range(pieces_of(b))]
-        assert len(small_loads) <= len(big_loads) // 2 * SMALL_LOADS_PER_PAIR
         for n, (b, s) in enumerate(big_loads):
+            if (b, s) == (LEAD, 0):
+                for dst, src in small_loads:
+                    nc.sync.dma_start(out=dst, in_=src)
+                small_loads = []
             image = memory[b].rearrange("(p t) h w -> p t (h w)", t=PACK)
             part = slice(s * HW // pieces_of(b), (s + 1) * HW // pieces_of(b))
             nc.sync.dma_start(out=raw[b][:, :, part], in_=image[:, :, part])
             if n % 2 == 1:
-                first = n // 2 * SMALL_LOADS_PER_PAIR
-                for dst, src in small_loads[first : first + SMALL_LOADS_PER_PAIR]:
+                for dst, src in small_loads[:SMALL_LOADS_PER_PAIR]:
                     nc.sync.dma_start(out=dst, in_=src)
+                small_loads = small_loads[SMALL_LOADS_PER_PAIR:]
 
         grouped = {}
 
-        def regroup(b):
-            for j in range(MEMBERS):
-                grouped[b, j] = stage.tile([P, POOLED, PACK], BF16, align_bytes=64, name="grouped%d" % j)
-            by_member = raw[b][:].rearrange("p t (hh dh ww dw) -> p dh dw hh ww t", dh=2, ww=W // 2, dw=2)
-            for s in range(pieces_of(b)):
-                rows = slice(s * (H // 2) // pieces_of(b), (s + 1) * (H // 2) // pieces_of(b))
-                for j in range(MEMBERS):
-                    dh, dw = divmod(j, 2)
-                    copy = nc.vector.tensor_copy if j in EVEN_COLUMNS else nc.scalar.copy
-                    copy(
-                        out=grouped[b, j][:].rearrange("p (hh ww) t -> p hh ww t", ww=W // 2)[:, rows, :, :],
-                        in_=by_member[:, dh, dw, rows, :, :],
-                    )
-
-        def quantise(b, members):
-            for j in members:
-                nc.vector.quantize_mx(
-                    out=codes[b][:, j, :].bitcast(FP8X4),
-                    scales=scales[b][:, j, :],
-                    in_=grouped[b, j][:].rearrange("p c t -> p (c t)"),
+        def regroup(b, s, slices):
+            by_parity = raw[b][:].rearrange("p t (hh dh ww dw) -> p dh hh ww t dw", dh=2, ww=W // 2, dw=2)
+            rows = slice(s * (H // 2) // slices, (s + 1) * (H // 2) // slices)
+            for dh in (EVEN_ROWS, ODD_ROWS):
+                if s == 0:
+                    grouped[b, dh] = stage.tile([P, 2, POOLED, PACK], BF16, align_bytes=64, name="grouped%d" % dh)
+                copy = nc.vector.tensor_copy if dh == EVEN_ROWS else nc.scalar.copy
+                copy(
+                    out=grouped[b, dh][:].rearrange("p dw (hh ww) t -> p hh ww t dw", ww=W // 2)[:, rows, :, :, :],
+                    in_=by_parity[:, dh, rows, :, :, :],
                 )
+
+        def quantise(b, dh):
+            both = slice(2 * dh * POOLED, (2 * dh + 2) * POOLED)
+            nc.vector.quantize_mx(
+                out=codes[b][:].rearrange("p j c -> p (j c)")[:, both].bitcast(FP8X4),
+                scales=scales[b][:].rearrange("p j c -> p (j c)")[:, both],
+                in_=grouped[b, dh][:].rearrange("p dw c t -> p (dw c t)"),
+            )
 
         def batch_norm_constants():
             vectors_f32 = keep.tile([P, P], F32)
@@ -151,7 +151,6 @@ def tile_selfattention_pa_t_kernel(
 
         zq = {}
         pooled = {}
-        ordered = {}
 
         def multiply(b, j):
             for g in range(GROUPS):
@@ -165,32 +164,18 @@ def tile_selfattention_pa_t_kernel(
                     start=True,
                     stop=True,
                 )
+                y = acc[:] if g == K else acc[:].rearrange("c (u r) -> c r u", r=R)
                 if g == Q:
                     zq[b, j] = results.tile([P, R, P], F32, name="zq", bufs=4)
-                    nc.scalar.activation(
-                        out=zq[b, j][:].rearrange("c r u -> c u r"),
-                        in_=acc[:].rearrange("c (u r) -> c u r", r=R),
-                        func=FUNC.Identity,
-                        scale=inv[:, g : g + 1],
-                        bias=shift[:, g : g + 1],
-                    )
-                elif j == 0:
-                    pooled[b, g] = results.tile([P, POOLED], F32, name="pooled%d" % g)
-                    nc.scalar.activation(out=pooled[b, g][:], in_=acc[:], func=FUNC.Copy, scale=inv[:, g : g + 1])
-                elif j < MEMBERS - 1 or g == K:
-                    nc.vector.scalar_tensor_tensor(
-                        out=pooled[b, g][:], in0=acc[:], scalar=inv[:, g : g + 1], in1=pooled[b, g][:], op0=ALU.mult, op1=ALU.max
-                    )
+                    nc.scalar.activation(out=zq[b, j][:], in_=y, func=FUNC.Identity, scale=inv[:, g : g + 1], bias=shift[:, g : g + 1])
                 else:
-                    ordered[b, g] = results.tile([P, R, P], F32, name="ordered%d" % g)
-                    nc.vector.scalar_tensor_tensor(
-                        out=ordered[b, g][:].rearrange("c r u -> c u r"),
-                        in0=acc[:].rearrange("c (u r) -> c u r", r=R),
-                        scalar=inv[:, g : g + 1],
-                        in1=pooled[b, g][:].rearrange("c (u r) -> c u r", r=R),
-                        op0=ALU.mult,
-                        op1=ALU.max,
-                    )
+                    if j == 0:
+                        pooled[b, g] = results.tile([P, POOLED], F32, name="pooled%d" % g)
+                    best = pooled[b, g][:] if g == K else pooled[b, g][:].rearrange("c (r u) -> c r u", r=R)
+                    if j == 0:
+                        nc.scalar.activation(out=best, in_=y, func=FUNC.Copy, scale=inv[:, g : g + 1])
+                    else:
+                        nc.vector.scalar_tensor_tensor(out=best, in0=y, scalar=inv[:, g : g + 1], in1=best, op0=ALU.mult, op1=ALU.max)
 
         def store_q(b, dh):
             q_out = results.tile([P, R, 2, P], F32)
@@ -215,7 +200,7 @@ def tile_selfattention_pa_t_kernel(
                     for half, g in enumerate((V_LOW, V_HIGH)):
                         nc.tensor.transpose(
                             turned[:, i, half * P : (half + 1) * P],
-                            ordered[b, g][:, 2 * pair + i, :],
+                            pooled[b, g][:, (2 * pair + i) * P : (2 * pair + i + 1) * P],
                             ident[:],
                         )
                 nc.vector.tensor_tensor(
@@ -227,27 +212,31 @@ def tile_selfattention_pa_t_kernel(
             nc.sync.dma_start(out=out_2[b].rearrange("(u r) c -> u (r c)", r=R), in_=v_out[:].rearrange("u r c -> u (r c)"))
 
         def produce(b):
-            multiply(b, 0)
-            if b > 0:
-                store_q(b - 1, 1)
-            multiply(b, 1)
-            if b > 0:
-                store_v(b - 1)
-            multiply(b, 2)
-            store_q(b, 0)
-            multiply(b, 3)
-            store_k(b)
+            for j in range(MEMBERS):
+                multiply(b, j)
+                if j == 0 and b + LEAD - 1 < B:
+                    quantise(b + LEAD - 1, ODD_ROWS)
+                if j == 0 and b > 0:
+                    store_q(b - 1, 1)
+                if j == 1 and b > 0:
+                    store_v(b - 1)
+                if j == 2:
+                    store_q(b, 0)
+                if j == 3:
+                    store_k(b)
+                if b + LEAD < B:
+                    regroup(b + LEAD, j, MEMBERS)
+            if b + LEAD < B:
+                quantise(b + LEAD, EVEN_ROWS)
 
-        for step in range(B + LEAD):
-            if step == LEAD:
-                inv, shift, shift_v = batch_norm_constants()
-            if step >= LEAD:
-                produce(step - LEAD)
-            if step < B:
-                regroup(step)
-            if 1 <= step <= B:
-                quantise(step - 1, ODD_COLUMNS)
-            if step < B:
-                quantise(step, EVEN_COLUMNS)
+        for b in range(LEAD):
+            for s in range(pieces_of(b)):
+                regroup(b, s, pieces_of(b))
+            if b > 0:
+                quantise(b - 1, ODD_ROWS)
+            quantise(b, EVEN_ROWS)
+        inv, shift, shift_v = batch_norm_constants()
+        for b in range(B):
+            produce(b)
         store_q(B - 1, 1)
         store_v(B - 1)

@@ -28,6 +28,7 @@ PIECES = 2
 FIRST_IMAGE_PIECES = 4
 SMALL_LOADS_PER_PAIR = 6
 LEAD = 2
+SLICES = 4
 
 FLOPS = 2 * B * HW * CH * C_OUT
 
@@ -119,24 +120,30 @@ def tile_selfattention_pa_t_kernel(
                 in_=grouped[b, dh][:].rearrange("p dw c t -> p (dw c t)"),
             )
 
-        def batch_norm_constants():
-            vectors_f32 = keep.tile([P, P], F32)
+        vectors_f32 = keep.tile([P, P], F32)
+        bn = keep.tile([P, 5, GROUPS], F32)
+        bias, gain, beta, mean, var = (bn[:, kind, :] for kind in range(5))
+        inv = keep.tile([P, GROUPS], F32)
+        shift = keep.tile([P, GROUPS], F32)
+        shift_v = keep.tile([P, 2 * P], F32)
+        turned_vectors = psum_tp.tile([P, P], F32, tag="tp")
+        spread = psum_tp.tile([P, 2 * P], F32, tag="tp")
+
+        def constants_step_1():
             nc.vector.tensor_copy(out=vectors_f32[:], in_=vectors[:])
-            turned = psum_tp.tile([P, P], F32, tag="tp")
-            nc.tensor.transpose(turned[:], vectors_f32[:], ident[:])
-            bn = keep.tile([P, 5, GROUPS], F32)
-            nc.vector.tensor_copy(out=bn[:].rearrange("p k g -> p (k g)"), in_=turned[:, 0 : 5 * GROUPS])
-            bias, gain, beta, mean, var = (bn[:, kind, :] for kind in range(5))
-            inv = keep.tile([P, GROUPS], F32)
-            shift = keep.tile([P, GROUPS], F32)
+            nc.tensor.transpose(turned_vectors[:], vectors_f32[:], ident[:])
+
+        def constants_step_2():
+            nc.vector.tensor_copy(out=bn[:].rearrange("p k g -> p (k g)"), in_=turned_vectors[:, 0 : 5 * GROUPS])
             nc.vector.tensor_scalar_add(out=inv[:], in0=var, scalar1=EPS)
             nc.scalar.sqrt(out=inv[:], in_=inv[:])
+
+        def constants_step_3():
             nc.vector.reciprocal(out=inv[:], in_=inv[:])
             nc.vector.tensor_mul(out=inv[:], in0=inv[:], in1=gain)
             nc.vector.tensor_sub(out=shift[:], in0=bias, in1=mean)
             nc.vector.tensor_mul(out=shift[:], in0=shift[:], in1=inv[:])
             nc.vector.tensor_add(out=shift[:], in0=shift[:], in1=beta)
-            spread = psum_tp.tile([P, 2 * P], F32, tag="tp")
             for half, g in enumerate((V_LOW, V_HIGH)):
                 nc.tensor.matmul(
                     out=spread[:, half * P : (half + 1) * P],
@@ -145,15 +152,15 @@ def tile_selfattention_pa_t_kernel(
                     start=True,
                     stop=True,
                 )
-            shift_v = keep.tile([P, 2 * P], F32)
+
+        def constants_step_4():
             nc.vector.tensor_copy(out=shift_v[:], in_=spread[:])
-            return inv, shift, shift_v
 
         zq = {}
         pooled = {}
 
         def multiply(b, j):
-            for g in range(GROUPS):
+            for g in (Q, V_LOW, V_HIGH, K):
                 acc = psum_acc.tile([P, POOLED], F32, tag="acc")
                 nc.tensor.matmul_mx(
                     out=acc[:],
@@ -179,14 +186,17 @@ def tile_selfattention_pa_t_kernel(
 
         def store_q(b, dh):
             q_out = results.tile([P, R, 2, P], F32)
+            q_rows = out_0[b].rearrange("(hh dh wq x) c -> dh hh wq (x c)", dh=2, wq=W // 8, x=8)
             for pair in range(R // 2):
                 turned = psum_tp.tile([P, 2, 2, P], F32, tag="tp")
                 for i in range(2):
                     for dw in range(2):
                         nc.tensor.transpose(turned[:, i, dw, :], zq[b, 2 * dh + dw][:, 2 * pair + i, :], ident[:])
                 nc.scalar.copy(out=q_out[:, 2 * pair : 2 * pair + 2, :, :], in_=turned[:])
-            q_rows = out_0[b].rearrange("(hh dh wq x) c -> dh hh wq (x c)", dh=2, wq=W // 8, x=8)
-            nc.sync.dma_start(out=q_rows[dh], in_=q_out[:].rearrange("u r d c -> u (r d c)"))
+                nc.sync.dma_start(
+                    out=q_rows[dh, :, :, pair * 4 * P : (pair + 1) * 4 * P],
+                    in_=q_out[:, 2 * pair : 2 * pair + 2, :, :].rearrange("u r d c -> u (r d c)"),
+                )
 
         def store_k(b):
             nc.vector.tensor_scalar_add(out=pooled[b, K][:], in0=pooled[b, K][:], scalar1=shift[:, K : K + 1])
@@ -194,6 +204,7 @@ def tile_selfattention_pa_t_kernel(
 
         def store_v(b):
             v_out = results.tile([P, R, 2 * P], F32)
+            v_rows = out_2[b].rearrange("(u r) c -> u (r c)", r=R)
             for pair in range(R // 2):
                 turned = psum_tp.tile([P, 2, 2 * P], F32, tag="tp")
                 for i in range(2):
@@ -209,13 +220,23 @@ def tile_selfattention_pa_t_kernel(
                     in1=shift_v[:].unsqueeze(1).to_broadcast([P, 2, 2 * P]),
                     op=ALU.add,
                 )
-            nc.sync.dma_start(out=out_2[b].rearrange("(u r) c -> u (r c)", r=R), in_=v_out[:].rearrange("u r c -> u (r c)"))
+                nc.sync.dma_start(
+                    out=v_rows[:, pair * 4 * P : (pair + 1) * 4 * P],
+                    in_=v_out[:, 2 * pair : 2 * pair + 2, :].rearrange("u r c -> u (r c)"),
+                )
+
+        def prepare(slot):
+            b, s = LEAD + slot // SLICES, slot % SLICES
+            if s == 0:
+                quantise(b - 1, ODD_ROWS)
+            if b < B:
+                regroup(b, s, SLICES)
+                if s == SLICES - 1:
+                    quantise(b, EVEN_ROWS)
 
         def produce(b):
             for j in range(MEMBERS):
                 multiply(b, j)
-                if j == 0 and b + LEAD - 1 < B:
-                    quantise(b + LEAD - 1, ODD_ROWS)
                 if j == 0 and b > 0:
                     store_q(b - 1, 1)
                 if j == 1 and b > 0:
@@ -224,18 +245,21 @@ def tile_selfattention_pa_t_kernel(
                     store_q(b, 0)
                 if j == 3:
                     store_k(b)
-                if b + LEAD < B:
-                    regroup(b + LEAD, j, MEMBERS)
-            if b + LEAD < B:
-                quantise(b + LEAD, EVEN_ROWS)
+                if j < MEMBERS - 1 and b < B - 1:
+                    prepare((MEMBERS - 1) * b + j)
 
-        for b in range(LEAD):
-            for s in range(pieces_of(b)):
-                regroup(b, s, pieces_of(b))
-            if b > 0:
-                quantise(b - 1, ODD_ROWS)
-            quantise(b, EVEN_ROWS)
-        inv, shift, shift_v = batch_norm_constants()
+        assert LEAD == 2 and (B - LEAD) * SLICES + 1 == (B - 1) * (MEMBERS - 1)
+        for s in range(FIRST_IMAGE_PIECES):
+            regroup(0, s, FIRST_IMAGE_PIECES)
+        quantise(0, EVEN_ROWS)
+        constants_step_1()
+        regroup(1, 0, PIECES)
+        constants_step_2()
+        regroup(1, 1, PIECES)
+        constants_step_3()
+        quantise(0, ODD_ROWS)
+        quantise(1, EVEN_ROWS)
+        constants_step_4()
         for b in range(B):
             produce(b)
         store_q(B - 1, 1)

@@ -46,8 +46,8 @@ def tile_selfattention_pa_t_kernel(
         keep = ctx.enter_context(tc.tile_pool(name="keep", bufs=1))
         stage = ctx.enter_context(tc.tile_pool(name="stage", bufs=2))
         results = ctx.enter_context(tc.tile_pool(name="results", bufs=3))
-        psum_acc = ctx.enter_context(tc.psum_pool(name="psum_acc", bufs=5))
-        psum_tp = ctx.enter_context(tc.psum_pool(name="psum_tp", bufs=3))
+        psum_acc = ctx.enter_context(tc.psum_pool(name="psum_acc", bufs=6))
+        psum_tp = ctx.enter_context(tc.psum_pool(name="psum_tp", bufs=2))
         ctx.enter_context(tc.manual_schedule())
 
         raw = [keep.tile([P, PACK, HW], BF16, name="raw%d" % b) for b in range(B)]
@@ -75,7 +75,7 @@ def tile_selfattention_pa_t_kernel(
             nc.gpsimd.dma_start(out=dst, in_=src)
         make_identity(nc, ident[:])
         small_loads = vector_loads[SMALL_LOADS_PER_PAIR:]
-        for words, scale_rows, first, width in ((wq_words, wq_scales, 0, P), (wk_words, wk_scales, P, P), (wv_words, wv_scales, 2 * P, 2 * P)):
+        for words, scale_rows, first, width in ((wq_words, wq_scales, 0, P), (wv_words, wv_scales, 2 * P, 2 * P), (wk_words, wk_scales, P, P)):
             cols = slice(first, first + width)
             small_loads.append((w_codes[:, cols].bitcast(I32), words[0].rearrange("p n t -> p (n t)").bitcast(I32)))
             for a in range(4):
@@ -84,19 +84,22 @@ def tile_selfattention_pa_t_kernel(
         def pieces_of(b):
             return FIRST_IMAGE_PIECES if b == 0 else PIECES
 
-        big_loads = [(b, s) for b in range(B) for s in range(pieces_of(b))]
-        for n, (b, s) in enumerate(big_loads):
-            if (b, s) == (LEAD, 0):
-                for dst, src in small_loads:
-                    nc.sync.dma_start(out=dst, in_=src)
-                small_loads = []
+        def load(b, s):
             image = memory[b].rearrange("(p t) h w -> p t (h w)", t=PACK)
             part = slice(s * HW // pieces_of(b), (s + 1) * HW // pieces_of(b))
             nc.sync.dma_start(out=raw[b][:, :, part], in_=image[:, :, part])
+
+        early = [(b, s) for b in range(LEAD) for s in range(pieces_of(b))]
+        for n, (b, s) in enumerate(early):
+            load(b, s)
             if n % 2 == 1:
-                for dst, src in small_loads[:SMALL_LOADS_PER_PAIR]:
+                for dst, src in small_loads[n // 2 * SMALL_LOADS_PER_PAIR : (n // 2 + 1) * SMALL_LOADS_PER_PAIR]:
                     nc.sync.dma_start(out=dst, in_=src)
-                small_loads = small_loads[SMALL_LOADS_PER_PAIR:]
+        for dst, src in small_loads[len(early) // 2 * SMALL_LOADS_PER_PAIR :]:
+            nc.sync.dma_start(out=dst, in_=src)
+        for b in range(LEAD, B):
+            for s in range(pieces_of(b)):
+                load(b, s)
 
         grouped = {}
 

@@ -33,6 +33,10 @@ SLICES = 4
 FLOPS = 2 * B * HW * CH * C_OUT
 
 
+def pieces_of(b):
+    return FIRST_IMAGE_PIECES if b == 0 else PIECES
+
+
 def tile_selfattention_pa_t_kernel(
     tc,
     memory,
@@ -50,7 +54,10 @@ def tile_selfattention_pa_t_kernel(
         psum_tp = ctx.enter_context(tc.psum_pool(name="psum_tp", bufs=2))
         ctx.enter_context(tc.manual_schedule())
 
-        raw = [keep.tile([P, PACK, HW], BF16, name="raw%d" % b) for b in range(B)]
+        raw = [
+            [keep.tile([P, PACK, HW // pieces_of(b)], BF16, name="raw%d_%d" % (b, s)) for s in range(pieces_of(b))]
+            for b in range(B)
+        ]
         codes = [keep.tile([P, MEMBERS, POOLED], U32, align_bytes=64, name="codes%d" % b) for b in range(B)]
         scales = [keep.tile([P, MEMBERS, POOLED], U8, align_bytes=64, name="scales%d" % b) for b in range(B)]
         w_codes = keep.tile([P, C_OUT], U32, align_bytes=64)
@@ -81,13 +88,10 @@ def tile_selfattention_pa_t_kernel(
             for a in range(4):
                 small_loads.append((w_scales[32 * a : 32 * a + 4, cols].bitcast(I32), scale_rows[0, 4 * a : 4 * a + 4, :].bitcast(I32)))
 
-        def pieces_of(b):
-            return FIRST_IMAGE_PIECES if b == 0 else PIECES
-
         def load(b, s):
             image = memory[b].rearrange("(p t) h w -> p t (h w)", t=PACK)
             part = slice(s * HW // pieces_of(b), (s + 1) * HW // pieces_of(b))
-            nc.sync.dma_start(out=raw[b][:, :, part], in_=image[:, :, part])
+            nc.sync.dma_start(out=raw[b][s][:], in_=image[:, :, part])
 
         early = [(b, s) for b in range(LEAD) for s in range(pieces_of(b))]
         for n, (b, s) in enumerate(early):
@@ -104,15 +108,16 @@ def tile_selfattention_pa_t_kernel(
         grouped = {}
 
         def regroup(b, s, slices):
-            by_parity = raw[b][:].rearrange("p t (hh dh ww dw) -> p dh hh ww t dw", dh=2, ww=W // 2, dw=2)
-            rows = slice(s * (H // 2) // slices, (s + 1) * (H // 2) // slices)
+            height = (H // 2) // slices
+            piece, top = divmod(s * height, (H // 2) // pieces_of(b))
+            by_parity = raw[b][piece][:].rearrange("p t (hh dh ww dw) -> p dh hh ww t dw", dh=2, ww=W // 2, dw=2)
             for dh in (EVEN_ROWS, ODD_ROWS):
                 if s == 0:
                     grouped[b, dh] = stage.tile([P, 2, POOLED, PACK], BF16, align_bytes=64, name="grouped%d" % dh)
                 copy = nc.vector.tensor_copy if dh == EVEN_ROWS else nc.scalar.copy
                 copy(
-                    out=grouped[b, dh][:].rearrange("p dw (hh ww) t -> p hh ww t dw", ww=W // 2)[:, rows, :, :, :],
-                    in_=by_parity[:, dh, rows, :, :, :],
+                    out=grouped[b, dh][:].rearrange("p dw (hh ww) t -> p hh ww t dw", ww=W // 2)[:, s * height : (s + 1) * height, :, :, :],
+                    in_=by_parity[:, dh, top : top + height, :, :, :],
                 )
 
         def quantise(b, dh):

@@ -28,7 +28,7 @@ PIECES = 2
 FIRST_IMAGE_PIECES = 4
 SMALL_LOADS_PER_PAIR = 6
 LEAD = 2
-SLICES = 4
+POOLED_ROWS = H // 2
 
 FLOPS = 2 * B * HW * CH * C_OUT
 
@@ -48,7 +48,6 @@ def tile_selfattention_pa_t_kernel(
     nc = tc.nc
     with ExitStack() as ctx:
         keep = ctx.enter_context(tc.tile_pool(name="keep", bufs=1))
-        stage = ctx.enter_context(tc.tile_pool(name="stage", bufs=2))
         results = ctx.enter_context(tc.tile_pool(name="results", bufs=3))
         psum_acc = ctx.enter_context(tc.psum_pool(name="psum_acc", bufs=6))
         psum_tp = ctx.enter_context(tc.psum_pool(name="psum_tp", bufs=2))
@@ -56,6 +55,10 @@ def tile_selfattention_pa_t_kernel(
 
         raw = [
             [keep.tile([P, PACK, HW // pieces_of(b)], BF16, name="raw%d_%d" % (b, s)) for s in range(pieces_of(b))]
+            for b in range(B)
+        ]
+        grouped = [
+            [keep.tile([P, 2, POOLED, PACK], BF16, align_bytes=64, name="grouped%d_%d" % (b, dh)) for dh in range(2)]
             for b in range(B)
         ]
         codes = [keep.tile([P, MEMBERS, POOLED], U32, align_bytes=64, name="codes%d" % b) for b in range(B)]
@@ -105,27 +108,28 @@ def tile_selfattention_pa_t_kernel(
             for s in range(pieces_of(b)):
                 load(b, s)
 
-        grouped = {}
-
-        def regroup(b, s, slices):
-            height = (H // 2) // slices
-            piece, top = divmod(s * height, (H // 2) // pieces_of(b))
+        def regroup(engine, b, dh, first, count):
+            piece, top = divmod(first, POOLED_ROWS // pieces_of(b))
+            assert top + count <= POOLED_ROWS // pieces_of(b)
             by_parity = raw[b][piece][:].rearrange("p t (hh dh ww dw) -> p dh hh ww t dw", dh=2, ww=W // 2, dw=2)
-            for dh in (EVEN_ROWS, ODD_ROWS):
-                if s == 0:
-                    grouped[b, dh] = stage.tile([P, 2, POOLED, PACK], BF16, align_bytes=64, name="grouped%d" % dh)
-                copy = nc.vector.tensor_copy if dh == EVEN_ROWS else nc.scalar.copy
-                copy(
-                    out=grouped[b, dh][:].rearrange("p dw (hh ww) t -> p hh ww t dw", ww=W // 2)[:, s * height : (s + 1) * height, :, :, :],
-                    in_=by_parity[:, dh, top : top + height, :, :, :],
-                )
+            dst = grouped[b][dh][:].rearrange("p dw (hh ww) t -> p hh ww t dw", ww=W // 2)[:, first : first + count, :, :, :]
+            src = by_parity[:, dh, top : top + count, :, :, :]
+            if engine == "vector":
+                nc.vector.tensor_copy(out=dst, in_=src)
+            elif engine == "scalar":
+                nc.scalar.copy(out=dst, in_=src)
+            else:
+                for dw in range(2):
+                    nc.gpsimd.tensor_scalar(
+                        out=dst[:, :, :, :, dw], in0=src[:, :, :, :, dw], scalar1=1.0, scalar2=0.0, op0=ALU.mult, op1=ALU.add
+                    )
 
         def quantise(b, dh):
             both = slice(2 * dh * POOLED, (2 * dh + 2) * POOLED)
             nc.vector.quantize_mx(
                 out=codes[b][:].rearrange("p j c -> p (j c)")[:, both].bitcast(FP8X4),
                 scales=scales[b][:].rearrange("p j c -> p (j c)")[:, both],
-                in_=grouped[b, dh][:].rearrange("p dw c t -> p (dw c t)"),
+                in_=grouped[b][dh][:].rearrange("p dw c t -> p (dw c t)"),
             )
 
         vectors_f32 = keep.tile([P, P], F32)
@@ -233,14 +237,10 @@ def tile_selfattention_pa_t_kernel(
                     in_=v_out[:, 2 * pair : 2 * pair + 2, :].rearrange("u r c -> u (r c)"),
                 )
 
-        def prepare(slot):
-            b, s = LEAD + slot // SLICES, slot % SLICES
-            if s == 0:
-                quantise(b - 1, ODD_ROWS)
-            if b < B:
-                regroup(b, s, SLICES)
-                if s == SLICES - 1:
-                    quantise(b, EVEN_ROWS)
+        for b in range(LEAD, B):
+            for dh in (EVEN_ROWS, ODD_ROWS):
+                for first in range(0, POOLED_ROWS, 8):
+                    regroup("gpsimd", b, dh, first, 8)
 
         def produce(b):
             for j in range(MEMBERS):
@@ -253,17 +253,22 @@ def tile_selfattention_pa_t_kernel(
                     store_q(b, 0)
                 if j == 3:
                     store_k(b)
-                if j < MEMBERS - 1 and b < B - 1:
-                    prepare((MEMBERS - 1) * b + j)
+                half = (MEMBERS * b + j) // 2 + 1
+                if j % 2 == 0 and 2 * LEAD <= half < 2 * B:
+                    quantise(half // 2, half % 2)
+                if (b, j) == (0, 0):
+                    quantise(1, ODD_ROWS)
 
-        assert LEAD == 2 and (B - LEAD) * SLICES + 1 == (B - 1) * (MEMBERS - 1)
         for s in range(FIRST_IMAGE_PIECES):
-            regroup(0, s, FIRST_IMAGE_PIECES)
+            regroup("vector", 0, EVEN_ROWS, 4 * s, 4)
+            regroup("scalar", 0, ODD_ROWS, 4 * s, 4)
         quantise(0, EVEN_ROWS)
         constants_step_1()
-        regroup(1, 0, PIECES)
+        regroup("vector", 1, EVEN_ROWS, 0, 8)
+        regroup("scalar", 1, ODD_ROWS, 0, 8)
         constants_step_2()
-        regroup(1, 1, PIECES)
+        regroup("vector", 1, EVEN_ROWS, 8, 8)
+        regroup("scalar", 1, ODD_ROWS, 8, 8)
         constants_step_3()
         quantise(0, ODD_ROWS)
         quantise(1, EVEN_ROWS)

@@ -57,10 +57,7 @@ def tile_selfattention_pa_t_kernel(
             [keep.tile([P, PACK, HW // pieces_of(b)], BF16, name="raw%d_%d" % (b, s)) for s in range(pieces_of(b))]
             for b in range(B)
         ]
-        grouped = [
-            [keep.tile([P, 2, POOLED, PACK], BF16, align_bytes=64, name="grouped%d_%d" % (b, dh)) for dh in range(2)]
-            for b in range(B)
-        ]
+        grouped = {}
         codes = [keep.tile([P, MEMBERS, POOLED], U32, align_bytes=64, name="codes%d" % b) for b in range(B)]
         scales = [keep.tile([P, MEMBERS, POOLED], U8, align_bytes=64, name="scales%d" % b) for b in range(B)]
         w_codes = keep.tile([P, C_OUT], U32, align_bytes=64)
@@ -111,8 +108,11 @@ def tile_selfattention_pa_t_kernel(
         def regroup(engine, b, dh, first, count):
             piece, top = divmod(first, POOLED_ROWS // pieces_of(b))
             assert top + count <= POOLED_ROWS // pieces_of(b)
+            if (b, dh) not in grouped:
+                place = (2, 1) if (b, dh) == (3, 0) else (b, dh)
+                grouped[b, dh] = keep.tile([P, 2, POOLED, PACK], BF16, align_bytes=64, name="grouped%d_%d" % place)
             by_parity = raw[b][piece][:].rearrange("p t (hh dh ww dw) -> p dh hh ww t dw", dh=2, ww=W // 2, dw=2)
-            dst = grouped[b][dh][:].rearrange("p dw (hh ww) t -> p hh ww t dw", ww=W // 2)[:, first : first + count, :, :, :]
+            dst = grouped[b, dh][:].rearrange("p dw (hh ww) t -> p hh ww t dw", ww=W // 2)[:, first : first + count, :, :, :]
             src = by_parity[:, dh, top : top + count, :, :, :]
             if engine == "vector":
                 nc.vector.tensor_copy(out=dst, in_=src)
@@ -129,7 +129,7 @@ def tile_selfattention_pa_t_kernel(
             nc.vector.quantize_mx(
                 out=codes[b][:].rearrange("p j c -> p (j c)")[:, both].bitcast(FP8X4),
                 scales=scales[b][:].rearrange("p j c -> p (j c)")[:, both],
-                in_=grouped[b][dh][:].rearrange("p dw c t -> p (dw c t)"),
+                in_=grouped[b, dh][:].rearrange("p dw c t -> p (dw c t)"),
             )
 
         vectors_f32 = keep.tile([P, P], F32)
@@ -211,7 +211,7 @@ def tile_selfattention_pa_t_kernel(
                 )
 
         def store_k(b):
-            nc.vector.tensor_scalar_add(out=pooled[b, K][:], in0=pooled[b, K][:], scalar1=shift[:, K : K + 1])
+            nc.scalar.activation(out=pooled[b, K][:], in_=pooled[b, K][:], func=FUNC.Identity, bias=shift[:, K : K + 1])
             nc.sync.dma_start(out=out_1[b], in_=pooled[b, K][:])
 
         def store_v(b):
@@ -237,10 +237,9 @@ def tile_selfattention_pa_t_kernel(
                     in_=v_out[:, 2 * pair : 2 * pair + 2, :].rearrange("u r c -> u (r c)"),
                 )
 
-        for b in range(LEAD, B):
-            for dh in (EVEN_ROWS, ODD_ROWS):
-                for first in range(0, POOLED_ROWS, 8):
-                    regroup("gpsimd", b, dh, first, 8)
+        def regroup_on_gpsimd(b, dh):
+            for first in range(0, POOLED_ROWS, 8):
+                regroup("gpsimd", b, dh, first, 8)
 
         def produce(b):
             for j in range(MEMBERS):
@@ -253,12 +252,21 @@ def tile_selfattention_pa_t_kernel(
                     store_q(b, 0)
                 if j == 3:
                     store_k(b)
-                half = (MEMBERS * b + j) // 2 + 1
-                if j % 2 == 0 and 2 * LEAD <= half < 2 * B:
-                    quantise(half // 2, half % 2)
                 if (b, j) == (0, 0):
                     quantise(1, ODD_ROWS)
+                if (b, j) == (1, 2):
+                    quantise(2, EVEN_ROWS)
+                    quantise(2, ODD_ROWS)
+                    regroup_on_gpsimd(3, EVEN_ROWS)
+                if (b, j) == (2, 2):
+                    quantise(3, EVEN_ROWS)
+                if (b, j) == (3, 0):
+                    quantise(3, ODD_ROWS)
+                if b in (1, 2):
+                    regroup("scalar", 3, ODD_ROWS, 2 * (MEMBERS * (b - 1) + j), 2)
 
+        regroup_on_gpsimd(2, EVEN_ROWS)
+        regroup_on_gpsimd(2, ODD_ROWS)
         for s in range(FIRST_IMAGE_PIECES):
             regroup("vector", 0, EVEN_ROWS, 4 * s, 4)
             regroup("scalar", 0, ODD_ROWS, 4 * s, 4)

@@ -245,13 +245,12 @@ def tile_selfattention_pa_t_kernel(
             for j in range(MEMBERS):
                 multiply(b, j)
                 if j == 0 and b > 0:
+                    store_k(b - 1)
                     store_q(b - 1, 1)
                 if j == 1 and b > 0:
                     store_v(b - 1)
                 if j == 2:
                     store_q(b, 0)
-                if j == 3:
-                    store_k(b)
                 if (b, j) == (0, 0):
                     quantise(1, ODD_ROWS)
                 if (b, j) == (1, 2):
@@ -284,4 +283,5 @@ def tile_selfattention_pa_t_kernel(
         for b in range(B):
             produce(b)
         store_q(B - 1, 1)
+        store_k(B - 1)
         store_v(B - 1)

@@ -65,6 +65,7 @@ def tile_selfattention_pa_t_kernel(
         vectors = keep.tile([P, P], BF16)
         ident = keep.tile([P, P], F32)
         one = keep.tile([P, 1], F32)
+        unused_max = keep.tile([P, 1], F32)
 
         nc.vector.memset(w_scales[:].bitcast(I32), 0)
         nc.vector.memset(vectors[:], 0.0)
@@ -78,10 +79,10 @@ def tile_selfattention_pa_t_kernel(
             vector_loads.append((vectors[row + Q : row + Q + 1, :], of_q.rearrange("(o c) -> o c", o=1)))
             vector_loads.append((vectors[row + K : row + K + 1, :], of_k.rearrange("(o c) -> o c", o=1)))
             vector_loads.append((vectors[row + V_LOW : row + V_HIGH + 1, :], of_v.rearrange("(o c) -> o c", o=2)))
-        for dst, src in vector_loads[:SMALL_LOADS_PER_PAIR]:
+        for dst, src in vector_loads[2 * SMALL_LOADS_PER_PAIR :]:
             nc.gpsimd.dma_start(out=dst, in_=src)
         make_identity(nc, ident[:])
-        small_loads = vector_loads[SMALL_LOADS_PER_PAIR:]
+        small_loads = vector_loads[: 2 * SMALL_LOADS_PER_PAIR]
         for words, scale_rows, first, width in ((wq_words, wq_scales, 0, P), (wv_words, wv_scales, 2 * P, 2 * P), (wk_words, wk_scales, P, P)):
             cols = slice(first, first + width)
             small_loads.append((w_codes[:, cols].bitcast(I32), words[0].rearrange("p n t -> p (n t)").bitcast(I32)))
@@ -93,15 +94,16 @@ def tile_selfattention_pa_t_kernel(
             part = slice(s * HW // pieces_of(b), (s + 1) * HW // pieces_of(b))
             nc.sync.dma_start(out=raw[b][s][:], in_=image[:, :, part])
 
-        early = [(b, s) for b in range(LEAD) for s in range(pieces_of(b))]
-        for n, (b, s) in enumerate(early):
-            load(b, s)
-            if n % 2 == 1:
-                for dst, src in small_loads[n // 2 * SMALL_LOADS_PER_PAIR : (n // 2 + 1) * SMALL_LOADS_PER_PAIR]:
+        for s in range(FIRST_IMAGE_PIECES):
+            load(0, s)
+            if s % 2 == 1:
+                for dst, src in small_loads[s // 2 * SMALL_LOADS_PER_PAIR : (s // 2 + 1) * SMALL_LOADS_PER_PAIR]:
                     nc.sync.dma_start(out=dst, in_=src)
-        for dst, src in small_loads[len(early) // 2 * SMALL_LOADS_PER_PAIR :]:
+        load(1, 0)
+        load(1, 1)
+        for dst, src in small_loads[FIRST_IMAGE_PIECES // 2 * SMALL_LOADS_PER_PAIR :]:
             nc.sync.dma_start(out=dst, in_=src)
-        for b in range(LEAD, B):
+        for b in range(2, B):
             for s in range(pieces_of(b)):
                 load(b, s)
 
@@ -211,7 +213,9 @@ def tile_selfattention_pa_t_kernel(
                 )
 
         def store_k(b):
-            nc.scalar.activation(out=pooled[b, K][:], in_=pooled[b, K][:], func=FUNC.Identity, bias=shift[:, K : K + 1])
+            nc.vector.tensor_scalar(
+                out=pooled[b, K][:], in0=pooled[b, K][:], scalar1=shift[:, K : K + 1], scalar2=None, op0=ALU.add, op1=ALU.max, accum_out=unused_max[:]
+            )
             nc.sync.dma_start(out=out_1[b], in_=pooled[b, K][:])
 
         def store_v(b):
@@ -237,20 +241,21 @@ def tile_selfattention_pa_t_kernel(
                     in_=v_out[:, 2 * pair : 2 * pair + 2, :].rearrange("u r c -> u (r c)"),
                 )
 
-        def regroup_on_gpsimd(b, dh):
-            for first in range(0, POOLED_ROWS, 8):
+        def regroup_on_gpsimd(b, dh, rows=POOLED_ROWS):
+            for first in range(0, rows, 8):
                 regroup("gpsimd", b, dh, first, 8)
 
         def produce(b):
             for j in range(MEMBERS):
                 multiply(b, j)
                 if j == 0 and b > 0:
-                    store_k(b - 1)
                     store_q(b - 1, 1)
                 if j == 1 and b > 0:
                     store_v(b - 1)
                 if j == 2:
                     store_q(b, 0)
+                if j == 3:
+                    store_k(b)
                 if (b, j) == (0, 0):
                     quantise(1, ODD_ROWS)
                 if (b, j) == (1, 2):
@@ -261,27 +266,29 @@ def tile_selfattention_pa_t_kernel(
                     quantise(3, EVEN_ROWS)
                 if (b, j) == (3, 0):
                     quantise(3, ODD_ROWS)
-                if b in (1, 2):
-                    regroup("scalar", 3, ODD_ROWS, 2 * (MEMBERS * (b - 1) + j), 2)
+                r = MEMBERS * b + j
+                if 2 <= r <= 5:
+                    regroup("scalar", 2, ODD_ROWS, POOLED_ROWS // 2 + 2 * (r - 2), 2)
+                if 6 <= r <= 9:
+                    regroup("scalar", 3, ODD_ROWS, 4 * (r - 6), 4)
 
         regroup_on_gpsimd(2, EVEN_ROWS)
-        regroup_on_gpsimd(2, ODD_ROWS)
+        regroup_on_gpsimd(2, ODD_ROWS, POOLED_ROWS // 2)
         for s in range(FIRST_IMAGE_PIECES):
             regroup("vector", 0, EVEN_ROWS, 4 * s, 4)
             regroup("scalar", 0, ODD_ROWS, 4 * s, 4)
-        quantise(0, EVEN_ROWS)
         constants_step_1()
+        quantise(0, EVEN_ROWS)
+        constants_step_2()
         regroup("vector", 1, EVEN_ROWS, 0, 8)
         regroup("scalar", 1, ODD_ROWS, 0, 8)
-        constants_step_2()
-        regroup("vector", 1, EVEN_ROWS, 8, 8)
-        regroup("scalar", 1, ODD_ROWS, 8, 8)
         constants_step_3()
         quantise(0, ODD_ROWS)
-        quantise(1, EVEN_ROWS)
+        regroup("vector", 1, EVEN_ROWS, 8, 8)
+        regroup("scalar", 1, ODD_ROWS, 8, 8)
         constants_step_4()
+        quantise(1, EVEN_ROWS)
         for b in range(B):
             produce(b)
         store_q(B - 1, 1)
-        store_k(B - 1)
         store_v(B - 1)

@@ -213,9 +213,12 @@ def tile_selfattention_pa_t_kernel(
                 )
 
         def store_k(b):
-            nc.vector.tensor_scalar(
-                out=pooled[b, K][:], in0=pooled[b, K][:], scalar1=shift[:, K : K + 1], scalar2=None, op0=ALU.add, op1=ALU.max, accum_out=unused_max[:]
-            )
+            if b == B - 1:
+                nc.scalar.activation(out=pooled[b, K][:], in_=pooled[b, K][:], func=FUNC.Identity, bias=shift[:, K : K + 1])
+            else:
+                nc.vector.tensor_scalar(
+                    out=pooled[b, K][:], in0=pooled[b, K][:], scalar1=shift[:, K : K + 1], scalar2=None, op0=ALU.add, op1=ALU.max, accum_out=unused_max[:]
+                )
             nc.sync.dma_start(out=out_1[b], in_=pooled[b, K][:])
 
         def store_v(b):
@@ -254,7 +257,7 @@ def tile_selfattention_pa_t_kernel(
                     store_v(b - 1)
                 if j == 2:
                     store_q(b, 0)
-                if j == 3:
+                if j == 3 and b < B - 1:
                     store_k(b)
                 if (b, j) == (0, 0):
                     quantise(1, ODD_ROWS)
@@ -291,4 +294,5 @@ def tile_selfattention_pa_t_kernel(
         for b in range(B):
             produce(b)
         store_q(B - 1, 1)
+        store_k(B - 1)
         store_v(B - 1)

@@ -65,7 +65,6 @@ def tile_selfattention_pa_t_kernel(
         vectors = keep.tile([P, P], BF16)
         ident = keep.tile([P, P], F32)
         one = keep.tile([P, 1], F32)
-        unused_max = keep.tile([P, 1], F32)
 
         nc.vector.memset(w_scales[:].bitcast(I32), 0)
         nc.vector.memset(vectors[:], 0.0)
@@ -173,8 +172,8 @@ def tile_selfattention_pa_t_kernel(
         zq = {}
         pooled = {}
 
-        def multiply(b, j):
-            for g in (Q, V_LOW, V_HIGH, K):
+        def multiply(b, j, groups):
+            for g in groups:
                 acc = psum_acc.tile([P, POOLED], F32, tag="acc")
                 nc.tensor.matmul_mx(
                     out=acc[:],
@@ -191,22 +190,25 @@ def tile_selfattention_pa_t_kernel(
                     nc.scalar.activation(out=zq[b, j][:], in_=y, func=FUNC.Identity, scale=inv[:, g : g + 1], bias=shift[:, g : g + 1])
                 else:
                     if j == 0:
-                        pooled[b, g] = results.tile([P, POOLED], F32, name="pooled%d" % g)
+                        pooled[b, g] = results.tile([P, POOLED], F32, name="pooled%d" % g, bufs=B if g == K else 3)
                     best = pooled[b, g][:] if g == K else pooled[b, g][:].rearrange("c (r u) -> c r u", r=R)
                     if j == 0:
                         nc.scalar.activation(out=best, in_=y, func=FUNC.Copy, scale=inv[:, g : g + 1])
                     else:
                         nc.vector.scalar_tensor_tensor(out=best, in0=y, scalar=inv[:, g : g + 1], in1=best, op0=ALU.mult, op1=ALU.max)
 
+        def transpose_bank(last):
+            return psum_acc.tile([P, 4, P], F32, name="turned_last", tag="acc") if last else psum_tp.tile([P, 4, P], F32, name="turned", tag="tp")
+
         def store_q(b, dh):
             q_out = results.tile([P, R, 2, P], F32)
             q_rows = out_0[b].rearrange("(hh dh wq x) c -> dh hh wq (x c)", dh=2, wq=W // 8, x=8)
             for pair in range(R // 2):
-                turned = psum_tp.tile([P, 2, 2, P], F32, tag="tp")
+                turned = transpose_bank((b, dh) == (B - 1, ODD_ROWS))
                 for i in range(2):
                     for dw in range(2):
-                        nc.tensor.transpose(turned[:, i, dw, :], zq[b, 2 * dh + dw][:, 2 * pair + i, :], ident[:])
-                nc.scalar.copy(out=q_out[:, 2 * pair : 2 * pair + 2, :, :], in_=turned[:])
+                        nc.tensor.transpose(turned[:, 2 * i + dw, :], zq[b, 2 * dh + dw][:, 2 * pair + i, :], ident[:])
+                nc.scalar.copy(out=q_out[:, 2 * pair : 2 * pair + 2, :, :].rearrange("u r d c -> u (r d) c"), in_=turned[:])
                 nc.sync.dma_start(
                     out=q_rows[dh, :, :, pair * 4 * P : (pair + 1) * 4 * P],
                     in_=q_out[:, 2 * pair : 2 * pair + 2, :, :].rearrange("u r d c -> u (r d c)"),
@@ -216,8 +218,8 @@ def tile_selfattention_pa_t_kernel(
             if b == B - 1:
                 nc.scalar.activation(out=pooled[b, K][:], in_=pooled[b, K][:], func=FUNC.Identity, bias=shift[:, K : K + 1])
             else:
-                nc.vector.tensor_scalar(
-                    out=pooled[b, K][:], in0=pooled[b, K][:], scalar1=shift[:, K : K + 1], scalar2=None, op0=ALU.add, op1=ALU.max, accum_out=unused_max[:]
+                nc.gpsimd.tensor_scalar(
+                    out=pooled[b, K][:], in0=pooled[b, K][:], scalar1=one[:], scalar2=shift[:, K : K + 1], op0=ALU.mult, op1=ALU.add
                 )
             nc.sync.dma_start(out=out_1[b], in_=pooled[b, K][:])
 
@@ -225,17 +227,17 @@ def tile_selfattention_pa_t_kernel(
             v_out = results.tile([P, R, 2 * P], F32)
             v_rows = out_2[b].rearrange("(u r) c -> u (r c)", r=R)
             for pair in range(R // 2):
-                turned = psum_tp.tile([P, 2, 2 * P], F32, tag="tp")
+                turned = transpose_bank(b == B - 1)
                 for i in range(2):
                     for half, g in enumerate((V_LOW, V_HIGH)):
                         nc.tensor.transpose(
-                            turned[:, i, half * P : (half + 1) * P],
+                            turned[:, 2 * i + half, :],
                             pooled[b, g][:, (2 * pair + i) * P : (2 * pair + i + 1) * P],
                             ident[:],
                         )
                 nc.vector.tensor_tensor(
                     out=v_out[:, 2 * pair : 2 * pair + 2, :],
-                    in0=turned[:],
+                    in0=turned[:].rearrange("u (i h) c -> u i (h c)", i=2),
                     in1=shift_v[:].unsqueeze(1).to_broadcast([P, 2, 2 * P]),
                     op=ALU.add,
                 )
@@ -250,15 +252,19 @@ def tile_selfattention_pa_t_kernel(
 
         def produce(b):
             for j in range(MEMBERS):
-                multiply(b, j)
+                if b < B - 1 or j < 3:
+                    multiply(b, j, (Q,))
+                multiply(b, j, (V_LOW, V_HIGH, K))
+                if (b, j) == (B - 1, 2):
+                    multiply(b, 3, (Q,))
                 if j == 0 and b > 0:
                     store_q(b - 1, 1)
                 if j == 1 and b > 0:
                     store_v(b - 1)
                 if j == 2:
                     store_q(b, 0)
-                if j == 3 and b < B - 1:
-                    store_k(b)
+                if b == B - 1 and j < B - 1:
+                    store_k(j)
                 if (b, j) == (0, 0):
                     quantise(1, ODD_ROWS)
                 if (b, j) == (1, 2):

@@ -187,7 +187,10 @@ def tile_selfattention_pa_t_kernel(
                 y = acc[:] if g == K else acc[:].rearrange("c (u r) -> c r u", r=R)
                 if g == Q:
                     zq[b, j] = results.tile([P, R, P], F32, name="zq", bufs=4)
-                    nc.scalar.activation(out=zq[b, j][:], in_=y, func=FUNC.Identity, scale=inv[:, g : g + 1], bias=shift[:, g : g + 1])
+                    if j == 0 and b > 0:
+                        nc.vector.tensor_scalar(out=zq[b, j][:], in0=y, scalar1=inv[:, g : g + 1], scalar2=shift[:, g : g + 1], op0=ALU.mult, op1=ALU.add)
+                    else:
+                        nc.scalar.activation(out=zq[b, j][:], in_=y, func=FUNC.Identity, scale=inv[:, g : g + 1], bias=shift[:, g : g + 1])
                 else:
                     if j == 0:
                         pooled[b, g] = results.tile([P, POOLED], F32, name="pooled%d" % g, bufs=B if g == K else 3)
@@ -252,9 +255,7 @@ def tile_selfattention_pa_t_kernel(
 
         def produce(b):
             for j in range(MEMBERS):
-                if b < B - 1 or j < 3:
-                    multiply(b, j, (Q,))
-                multiply(b, j, (V_LOW, V_HIGH, K))
+                multiply(b, j, (V_LOW, Q, V_HIGH, K) if (b, j) != (B - 1, 3) else (V_LOW, V_HIGH, K))
                 if (b, j) == (B - 1, 2):
                     multiply(b, 3, (Q,))
                 if j == 0 and b > 0:

from contextlib import ExitStack

import concourse.mybir as mybir
from concourse.masks import make_identity

F32 = mybir.dt.float32
BF16 = mybir.dt.bfloat16
I32 = mybir.dt.int32
U32 = mybir.dt.uint32
U8 = mybir.dt.uint8
FP8X4 = mybir.dt.float8_e4m3fn_x4
ALU = mybir.AluOpType
FUNC = mybir.ActivationFunctionType

P = 128
PACK = 4
B, CH, H, W = 4, 512, 32, 64
HW = H * W
POOLED = HW // 4
MEMBERS = 4
EVEN_ROWS, ODD_ROWS = 0, 1
C_OUT = 512
GROUPS = C_OUT // P
Q, K, V_LOW, V_HIGH = 0, 1, 2, 3
R = POOLED // P
EPS = 1e-5
PIECES = 2
FIRST_IMAGE_PIECES = 4
SMALL_LOADS_PER_PAIR = 6
LEAD = 2
POOLED_ROWS = H // 2

FLOPS = 2 * B * HW * CH * C_OUT


def pieces_of(b):
    return FIRST_IMAGE_PIECES if b == 0 else PIECES


def tile_selfattention_pa_t_kernel(
    tc,
    memory,
    wq_words, wq_scales, bq, bnq_s, bnq_b, bnq_m, bnq_v,
    wk_words, wk_scales, bk, bnk_s, bnk_b, bnk_m, bnk_v,
    wv_words, wv_scales, bv, bnv_s, bnv_b, bnv_m, bnv_v,
    out_0, out_1, out_2,
):
    nc = tc.nc
    with ExitStack() as ctx:
        keep = ctx.enter_context(tc.tile_pool(name="keep", bufs=1))
        results = ctx.enter_context(tc.tile_pool(name="results", bufs=3))
        psum_acc = ctx.enter_context(tc.psum_pool(name="psum_acc", bufs=6))
        psum_tp = ctx.enter_context(tc.psum_pool(name="psum_tp", bufs=2))
        ctx.enter_context(tc.manual_schedule())

        raw = [
            [keep.tile([P, PACK, HW // pieces_of(b)], BF16, name="raw%d_%d" % (b, s)) for s in range(pieces_of(b))]
            for b in range(B)
        ]
        grouped = {}
        codes = [keep.tile([P, MEMBERS, POOLED], U32, align_bytes=64, name="codes%d" % b) for b in range(B)]
        scales = [keep.tile([P, MEMBERS, POOLED], U8, align_bytes=64, name="scales%d" % b) for b in range(B)]
        w_codes = keep.tile([P, C_OUT], U32, align_bytes=64)
        w_scales = keep.tile([P, C_OUT], U8, align_bytes=64)
        vectors = keep.tile([P, P], BF16)
        ident = keep.tile([P, P], F32)
        one = keep.tile([P, 1], F32)

        nc.vector.memset(w_scales[:].bitcast(I32), 0)
        nc.vector.memset(vectors[:], 0.0)
        nc.vector.memset(one[:], 1.0)
        nc.scalar.sqrt(out=one[:], in_=one[:])

        vector_loads = []
        by_kind = ((bq, bk, bv), (bnq_s, bnk_s, bnv_s), (bnq_b, bnk_b, bnv_b), (bnq_m, bnk_m, bnv_m), (bnq_v, bnk_v, bnv_v))
        for kind, (of_q, of_k, of_v) in enumerate(by_kind):
            row = GROUPS * kind
            vector_loads.append((vectors[row + Q : row + Q + 1, :], of_q.rearrange("(o c) -> o c", o=1)))
            vector_loads.append((vectors[row + K : row + K + 1, :], of_k.rearrange("(o c) -> o c", o=1)))
            vector_loads.append((vectors[row + V_LOW : row + V_HIGH + 1, :], of_v.rearrange("(o c) -> o c", o=2)))
        for dst, src in vector_loads[2 * SMALL_LOADS_PER_PAIR :]:
            nc.gpsimd.dma_start(out=dst, in_=src)
        make_identity(nc, ident[:])
        small_loads = vector_loads[: 2 * SMALL_LOADS_PER_PAIR]
        for words, scale_rows, first, width in ((wq_words, wq_scales, 0, P), (wv_words, wv_scales, 2 * P, 2 * P), (wk_words, wk_scales, P, P)):
            cols = slice(first, first + width)
            small_loads.append((w_codes[:, cols].bitcast(I32), words[0].rearrange("p n t -> p (n t)").bitcast(I32)))
            for a in range(4):
                small_loads.append((w_scales[32 * a : 32 * a + 4, cols].bitcast(I32), scale_rows[0, 4 * a : 4 * a + 4, :].bitcast(I32)))

        def load(b, s):
            image = memory[b].rearrange("(p t) h w -> p t (h w)", t=PACK)
            part = slice(s * HW // pieces_of(b), (s + 1) * HW // pieces_of(b))
            nc.sync.dma_start(out=raw[b][s][:], in_=image[:, :, part])

        for s in range(FIRST_IMAGE_PIECES):
            load(0, s)
            if s % 2 == 1:
                for dst, src in small_loads[s // 2 * SMALL_LOADS_PER_PAIR : (s // 2 + 1) * SMALL_LOADS_PER_PAIR]:
                    nc.sync.dma_start(out=dst, in_=src)
        load(1, 0)
        load(1, 1)
        for dst, src in small_loads[FIRST_IMAGE_PIECES // 2 * SMALL_LOADS_PER_PAIR :]:
            nc.sync.dma_start(out=dst, in_=src)
        for b in range(2, B):
            for s in range(pieces_of(b)):
                load(b, s)

        def regroup(engine, b, dh, first, count):
            piece, top = divmod(first, POOLED_ROWS // pieces_of(b))
            assert top + count <= POOLED_ROWS // pieces_of(b)
            if (b, dh) not in grouped:
                place = (2, 1) if (b, dh) == (3, 0) else (b, dh)
                grouped[b, dh] = keep.tile([P, 2, POOLED, PACK], BF16, align_bytes=64, name="grouped%d_%d" % place)
            by_parity = raw[b][piece][:].rearrange("p t (hh dh ww dw) -> p dh hh ww t dw", dh=2, ww=W // 2, dw=2)
            dst = grouped[b, dh][:].rearrange("p dw (hh ww) t -> p hh ww t dw", ww=W // 2)[:, first : first + count, :, :, :]
            src = by_parity[:, dh, top : top + count, :, :, :]
            if engine == "vector":
                nc.vector.tensor_copy(out=dst, in_=src)
            elif engine == "scalar":
                nc.scalar.copy(out=dst, in_=src)
            else:
                for dw in range(2):
                    nc.gpsimd.tensor_scalar(
                        out=dst[:, :, :, :, dw], in0=src[:, :, :, :, dw], scalar1=1.0, scalar2=0.0, op0=ALU.mult, op1=ALU.add
                    )

        def quantise(b, dh):
            both = slice(2 * dh * POOLED, (2 * dh + 2) * POOLED)
            nc.vector.quantize_mx(
                out=codes[b][:].rearrange("p j c -> p (j c)")[:, both].bitcast(FP8X4),
                scales=scales[b][:].rearrange("p j c -> p (j c)")[:, both],
                in_=grouped[b, dh][:].rearrange("p dw c t -> p (dw c t)"),
            )

        vectors_f32 = keep.tile([P, P], F32)
        bn = keep.tile([P, 5, GROUPS], F32)
        bias, gain, beta, mean, var = (bn[:, kind, :] for kind in range(5))
        inv = keep.tile([P, GROUPS], F32)
        shift = keep.tile([P, GROUPS], F32)
        shift_v = keep.tile([P, 2 * P], F32)
        turned_vectors = psum_tp.tile([P, P], F32, tag="tp")
        spread = psum_tp.tile([P, 2 * P], F32, tag="tp")

        def constants_step_1():
            nc.vector.tensor_copy(out=vectors_f32[:], in_=vectors[:])
            nc.tensor.transpose(turned_vectors[:], vectors_f32[:], ident[:])

        def constants_step_2():
            nc.vector.tensor_copy(out=bn[:].rearrange("p k g -> p (k g)"), in_=turned_vectors[:, 0 : 5 * GROUPS])
            nc.vector.tensor_scalar_add(out=inv[:], in0=var, scalar1=EPS)
            nc.scalar.sqrt(out=inv[:], in_=inv[:])

        def constants_step_3():
            nc.vector.reciprocal(out=inv[:], in_=inv[:])
            nc.vector.tensor_mul(out=inv[:], in0=inv[:], in1=gain)
            nc.vector.tensor_sub(out=shift[:], in0=bias, in1=mean)
            nc.vector.tensor_mul(out=shift[:], in0=shift[:], in1=inv[:])
            nc.vector.tensor_add(out=shift[:], in0=shift[:], in1=beta)
            for half, g in enumerate((V_LOW, V_HIGH)):
                nc.tensor.matmul(
                    out=spread[:, half * P : (half + 1) * P],
                    lhsT=shift[:, g : g + 1].to_broadcast([P, P]),
                    rhs=ident[:],
                    start=True,
                    stop=True,
                )

        def constants_step_4():
            nc.vector.tensor_copy(out=shift_v[:], in_=spread[:])

        zq = {}
        pooled = {}

        def multiply(b, j, groups):
            for g in groups:
                acc = psum_acc.tile([P, POOLED], F32, tag="acc")
                nc.tensor.matmul_mx(
                    out=acc[:],
                    lhsT=w_codes[:, g * P : (g + 1) * P].bitcast(FP8X4),
                    lhsT_scale=w_scales[:, g * P : (g + 1) * P],
                    rhs=codes[b][:, j, :].bitcast(FP8X4),
                    rhs_scale=scales[b][:, j, :],
                    start=True,
                    stop=True,
                )
                y = acc[:] if g == K else acc[:].rearrange("c (u r) -> c r u", r=R)
                if g == Q:
                    zq[b, j] = results.tile([P, R, P], F32, name="zq", bufs=4)
                    if j == 0 and b > 0:
                        nc.vector.tensor_scalar(out=zq[b, j][:], in0=y, scalar1=inv[:, g : g + 1], scalar2=shift[:, g : g + 1], op0=ALU.mult, op1=ALU.add)
                    else:
                        nc.scalar.activation(out=zq[b, j][:], in_=y, func=FUNC.Identity, scale=inv[:, g : g + 1], bias=shift[:, g : g + 1])
                else:
                    if j == 0:
                        pooled[b, g] = results.tile([P, POOLED], F32, name="pooled%d" % g, bufs=B if g == K else 3)
                    best = pooled[b, g][:] if g == K else pooled[b, g][:].rearrange("c (r u) -> c r u", r=R)
                    if j == 0:
                        nc.scalar.activation(out=best, in_=y, func=FUNC.Copy, scale=inv[:, g : g + 1])
                    else:
                        nc.vector.scalar_tensor_tensor(out=best, in0=y, scalar=inv[:, g : g + 1], in1=best, op0=ALU.mult, op1=ALU.max)

        def transpose_bank(last):
            return psum_acc.tile([P, 4, P], F32, name="turned_last", tag="acc") if last else psum_tp.tile([P, 4, P], F32, name="turned", tag="tp")

        def store_q(b, dh):
            q_out = results.tile([P, R, 2, P], F32)
            q_rows = out_0[b].rearrange("(hh dh wq x) c -> dh hh wq (x c)", dh=2, wq=W // 8, x=8)
            for pair in range(R // 2):
                turned = transpose_bank((b, dh) == (B - 1, ODD_ROWS))
                for i in range(2):
                    for dw in range(2):
                        nc.tensor.transpose(turned[:, 2 * i + dw, :], zq[b, 2 * dh + dw][:, 2 * pair + i, :], ident[:])
                nc.scalar.copy(out=q_out[:, 2 * pair : 2 * pair + 2, :, :].rearrange("u r d c -> u (r d) c"), in_=turned[:])
                nc.sync.dma_start(
                    out=q_rows[dh, :, :, pair * 4 * P : (pair + 1) * 4 * P],
                    in_=q_out[:, 2 * pair : 2 * pair + 2, :, :].rearrange("u r d c -> u (r d c)"),
                )

        def store_k(b):
            if b == B - 1:
                nc.scalar.activation(out=pooled[b, K][:], in_=pooled[b, K][:], func=FUNC.Identity, bias=shift[:, K : K + 1])
            else:
                nc.gpsimd.tensor_scalar(
                    out=pooled[b, K][:], in0=pooled[b, K][:], scalar1=one[:], scalar2=shift[:, K : K + 1], op0=ALU.mult, op1=ALU.add
                )
            nc.sync.dma_start(out=out_1[b], in_=pooled[b, K][:])

        def store_v(b):
            v_out = results.tile([P, R, 2 * P], F32)
            v_rows = out_2[b].rearrange("(u r) c -> u (r c)", r=R)
            for pair in range(R // 2):
                turned = transpose_bank(b == B - 1)
                for i in range(2):
                    for half, g in enumerate((V_LOW, V_HIGH)):
                        nc.tensor.transpose(
                            turned[:, 2 * i + half, :],
                            pooled[b, g][:, (2 * pair + i) * P : (2 * pair + i + 1) * P],
                            ident[:],
                        )
                nc.vector.tensor_tensor(
                    out=v_out[:, 2 * pair : 2 * pair + 2, :],
                    in0=turned[:].rearrange("u (i h) c -> u i (h c)", i=2),
                    in1=shift_v[:].unsqueeze(1).to_broadcast([P, 2, 2 * P]),
                    op=ALU.add,
                )
                nc.sync.dma_start(
                    out=v_rows[:, pair * 4 * P : (pair + 1) * 4 * P],
                    in_=v_out[:, 2 * pair : 2 * pair + 2, :].rearrange("u r c -> u (r c)"),
                )

        def regroup_on_gpsimd(b, dh, rows=POOLED_ROWS):
            for first in range(0, rows, 8):
                regroup("gpsimd", b, dh, first, 8)

        def produce(b):
            for j in range(MEMBERS):
                multiply(b, j, (V_LOW, Q, V_HIGH, K) if (b, j) != (B - 1, 3) else (V_LOW, V_HIGH, K))
                if (b, j) == (B - 1, 2):
                    multiply(b, 3, (Q,))
                if j == 0 and b > 0:
                    store_q(b - 1, 1)
                if j == 1 and b > 0:
                    store_v(b - 1)
                if j == 2:
                    store_q(b, 0)
                if b == B - 1 and j < B - 1:
                    store_k(j)
                if (b, j) == (0, 0):
                    quantise(1, ODD_ROWS)
                if (b, j) == (1, 2):
                    quantise(2, EVEN_ROWS)
                    quantise(2, ODD_ROWS)
                    regroup_on_gpsimd(3, EVEN_ROWS)
                if (b, j) == (2, 2):
                    quantise(3, EVEN_ROWS)
                if (b, j) == (3, 0):
                    quantise(3, ODD_ROWS)
                r = MEMBERS * b + j
                if 2 <= r <= 5:
                    regroup("scalar", 2, ODD_ROWS, POOLED_ROWS // 2 + 2 * (r - 2), 2)
                if 6 <= r <= 9:
                    regroup("scalar", 3, ODD_ROWS, 4 * (r - 6), 4)

        regroup_on_gpsimd(2, EVEN_ROWS)
        regroup_on_gpsimd(2, ODD_ROWS, POOLED_ROWS // 2)
        for s in range(FIRST_IMAGE_PIECES):
            regroup("vector", 0, EVEN_ROWS, 4 * s, 4)
            regroup("scalar", 0, ODD_ROWS, 4 * s, 4)
        constants_step_1()
        quantise(0, EVEN_ROWS)
        constants_step_2()
        regroup("vector", 1, EVEN_ROWS, 0, 8)
        regroup("scalar", 1, ODD_ROWS, 0, 8)
        constants_step_3()
        quantise(0, ODD_ROWS)
        regroup("vector", 1, EVEN_ROWS, 8, 8)
        regroup("scalar", 1, ODD_ROWS, 8, 8)
        constants_step_4()
        quantise(1, EVEN_ROWS)
        for b in range(B):
            produce(b)
        store_q(B - 1, 1)
        store_k(B - 1)
        store_v(B - 1)
